import numpy as np
import ml_dtypes


def mxq(x, axis, fmt="e4m3"):
    dtype, down = {"e4m3": (ml_dtypes.float8_e4m3fn, 7), "e5m2": (ml_dtypes.float8_e5m2, 14)}[fmt]
    v = np.moveaxis(np.asarray(x, np.float32).astype(ml_dtypes.bfloat16).astype(np.float64), axis, -1)
    blocks = v.reshape(v.shape[:-1] + (-1, 32))
    amax = np.abs(blocks).max(-1, keepdims=True)
    byte = np.maximum(np.where(amax > 0, np.frexp(amax)[1] - 1 + 127, 0) - down, 1)
    scale = np.exp2(byte - 127.0)
    codes = (blocks / scale).astype(np.float32).astype(dtype).astype(np.float64)
    return np.moveaxis((codes * scale).reshape(v.shape), -1, axis)


WIDE = False


def mx_kscale(k):
    if not WIDE:
        return np.ones(k)
    levels = np.array([10, -10, 5, -5, 0])
    if k % 512:
        return np.exp2(np.random.permutation(np.resize(levels, k // 32))).repeat(32)
    a = np.empty((k // 512, 16))
    for p in range(k // 512):
        a[p, :8] = np.random.permutation(np.resize(levels, 8))
        for g in range(8):
            far = levels[np.abs(levels - a[p, g]) >= 10]
            a[p, g + 8] = far[np.random.randint(len(far))]
    return np.exp2(a.ravel()).repeat(32)


BF16 = ml_dtypes.bfloat16


def bf(x):
    return np.asarray(x, np.float32).astype(BF16)


def f64(x):
    return np.asarray(x).astype(np.float64)


B, D0, D1, D2, D3 = 512, 2048, 2048, 2048, 2048
HEBB = 0.01
RATE = 0.001
BATCH_NUM = 1
C = HEBB * RATE / BATCH_NUM


def centred(s):
    return s / np.exp2(np.round(np.log2(s.mean())))


def setup_inputs():
    s, t = centred(mx_kscale(D0)), centred(mx_kscale(D1))
    return {"x": bf((4.0 + 3.0 * np.random.standard_normal((B, D0))) * s),
            "W1": bf(np.random.standard_normal((D1, D0)) * 0.9 / np.sqrt(D0) / s[None, :] * t[:, None]),
            "b1": bf((3.0 + 1.5 * np.random.standard_normal(D1)) * t),
            "W2": bf(np.random.standard_normal((D2, D1)) * 0.9 / np.sqrt(D1) / t[None, :]),
            "b2": bf(3.0 + 1.5 * np.random.standard_normal(D2))}


def reference(x, W1, b1, W2, b2):
    x = f64(x)
    v1 = np.maximum((mxq(x, 1, "e4m3") @ mxq(f64(W1), 1, "e4m3").T) + f64(b1), 0.0)
    m1 = np.mean(v1, axis=0)
    h = v1 + np.sum(x, axis=1, keepdims=True) * (C * m1)[None, :]
    v2 = np.maximum((mxq(h, 1, "e4m3") @ mxq(f64(W2), 1, "e4m3").T) + f64(b2), 0.0)
    m2 = np.mean(v2, axis=0)
    out = v2 + np.sum(h, axis=1, keepdims=True) * (C * m2)[None, :]
    return out, m1, m2

@@ -1,0 +1,400 @@
+from contextlib import ExitStack
+
+import concourse.mybir as mybir
+from concourse.masks import make_identity
+
+F32 = mybir.dt.float32
+BF16 = mybir.dt.bfloat16
+U32 = mybir.dt.uint32
+U8 = mybir.dt.uint8
+FP8X4 = mybir.dt.float8_e4m3fn_x4
+ACT = mybir.ActivationFunctionType
+ALU = mybir.AluOpType
+AX = mybir.AxisListType
+
+P = 128
+ROWS = 512
+C = 0.01 * 0.001 / 1
+FLOPS = 2 * 2 * 512 * 2048 * 2048
+
+NW = 6
+EW_ENG = ["SSSS", "SSSS"]
+EW0_ENG = "SVSV"
+ADDS_L2 = 5
+ADDS_8 = 3
+LAG = 2
+TO_PER_STEP = 2
+SH_DELAY = 3
+REP_ENG = "G"
+NV = 18
+WARM0 = 4
+WARM1 = 2
+AH = [1, 1, 1, 1, 1, 1, 1, 1, 1, 2]
+
+
+def tile_optimalnet_pa_kernel(tc, x, W1, b1, W2, b2, out_0, out_1, out_2):
+    nc = tc.nc
+    with ExitStack() as ctx:
+        const = ctx.enter_context(tc.tile_pool(name="const", bufs=1))
+        win = ctx.enter_context(tc.tile_pool(name="win", bufs=NW))
+        stage = ctx.enter_context(tc.tile_pool(name="stage", bufs=3))
+        work = ctx.enter_context(tc.tile_pool(name="work", bufs=2))
+        psT = ctx.enter_context(tc.psum_pool(name="psT", bufs=6))
+        psM = ctx.enter_context(tc.psum_pool(name="psM", bufs=2))
+        ctx.enter_context(tc.manual_schedule())
+
+        def copy_on(eng, out, in_):
+            if eng == "V":
+                nc.vector.tensor_copy(out=out, in_=in_)
+            else:
+                nc.scalar.copy(out=out, in_=in_)
+
+        xt = [win.tile([P, 4096], BF16, name="x0", tag="w"), win.tile([P, 4096], BF16, name="x1", tag="w")]
+        w0 = win.tile([P, 4096], BF16, name="w0", tag="w")
+
+        def load_x(rt, lo=0, hi=2048):
+            nc.sync.dma_start(out=xt[rt // 2][:, (rt % 2) * 2048 + lo:(rt % 2) * 2048 + hi], in_=x[rt * P:(rt + 1) * P, lo:hi])
+
+        def load_w0(e):
+            nc.sync.dma_start(out=w0[:, e * 2048:(e + 1) * 2048], in_=W1.rearrange("(g p h e) k -> g h p e k", p=P, h=2, e=2)[0][0][:, e, :])
+
+        load_x(0, 0, 1024)
+        load_x(0, 1024, 2048)
+        ones_b = const.tile([P, 512], BF16, name="ones_b")
+        nc.vector.memset(ones_b[:], 1.0)
+        bz = const.tile([P, 512], BF16, name="bz")
+        nc.vector.memset(bz[:], 0.0)
+        nc.sync.dma_start(out=bz[0:4, :], in_=b1.rearrange("(g n) -> g n", n=512))
+        nc.sync.dma_start(out=bz[4:12, 0:256], in_=b2.rearrange("(c n) -> c n", n=256))
+        load_x(1)
+        load_x(2)
+        load_w0(0)
+        load_x(3)
+        load_w0(1)
+        ident = const.tile([P, P], F32, name="ident")
+        make_identity(nc, ident[:])
+        ones_f = const.tile([P, P], F32, name="ones_f")
+        nc.vector.memset(ones_f[:], 1.0)
+        mp = [const.tile([P, 512], F32, name="mp0"), const.tile([P, 16], F32, name="mp1")]
+        nc.vector.memset(mp[0][:], 0.0)
+        tabl = const.tile([P, 1], F32, name="tabl")
+        nc.scalar.activation(out=tabl[:], in_=ones_f[:, 0:1], func=ACT.Relu)
+        warm = psT.tile([P, 512], F32, name="warm", tag="T")
+
+        def warm_up(n):
+            for i in range(n):
+                nc.tensor.matmul(out=warm[:], lhsT=ones_b[:, 0:P], rhs=ones_b[:], start=True, stop=True)
+
+        warm_up(WARM0)
+
+        gx = const.tile([P, 8192], BF16, name="gx", align_bytes=64)
+        xc = const.tile([P, 2048], U32, name="xc", align_bytes=64)
+        xsc = const.tile([P, 2048], U8, name="xsc", align_bytes=64)
+        hc = const.tile([P, 2048], U32, name="hc", align_bytes=64)
+        hsc = const.tile([P, 2048], U8, name="hsc", align_bytes=64)
+        bw = const.tile([P, 16], F32, name="bw")
+        biasf = const.tile([P, 32], F32, name="biasf")
+        sxr = const.tile([P, ROWS], F32, name="sxr")
+        sxc = const.tile([P, ROWS], F32, name="sxc")
+        acc = [const.tile([P, ROWS], F32, name="acc0"), const.tile([P, ROWS], F32, name="acc1")]
+        accf = const.tile([P, ROWS], F32, name="accf")
+        shc = const.tile([P, 4], F32, name="shc")
+        s1 = const.tile([P, 1], F32, name="s1")
+        m2b = const.tile([P, 2048], F32, name="m2b")
+
+        w1src = W1.rearrange("(g p h e) k -> g h p (e k)", p=P, h=2, e=2)
+        w2src = W2.rearrange("(c p e) k -> c p (e k)", p=P, e=2)
+        wt, tb, gw, wc, ws, mb, vt, ob, hcn, gh, rep = {}, {}, {}, {}, {}, {}, {}, {}, {}, {}, {}
+
+        def load(b):
+            t = win.tile([P, 4096], BF16, name="w%d" % b, tag="w")
+            nc.sync.dma_start(out=t[:], in_=w1src[b // 2][b % 2] if b < 8 else w2src[b - 8])
+            wt[b] = t
+
+        def four_transposes(bank, src32, cols):
+            for i in range(4):
+                nc.tensor.transpose(out=bank[:, i * P:(i + 1) * P], in_=src32[:, cols[i]:cols[i] + 255:2], identity=ident[:])
+
+        def tx(rt):
+            x32 = xt[rt // 2][:].bitcast(F32)
+            for gp in range(2):
+                bank = psT.tile([P, 512], F32, name="tx%d_%d" % (rt, gp), tag="T")
+                four_transposes(bank, x32, [(rt % 2) * 1024 + (2 * gp + gl) * 256 + u for gl in range(2) for u in range(2)])
+                tb[("x", rt, gp)] = bank
+
+        def ex(rt, gp, eng):
+            dst = gx[:].bitcast(F32).rearrange("p (g r u) -> p g r u", g=4, u=2)[:, 2 * gp:2 * gp + 2, rt * P:(rt + 1) * P, :]
+            copy_on(eng, dst, tb[("x", rt, gp)][:].rearrange("p (g u r) -> p g r u", g=2, u=2))
+
+        def qx(rt):
+            for g in range(4):
+                lo = g * 512 + rt * P
+                nc.vector.quantize_mx(out=xc[:, lo:lo + P].bitcast(FP8X4), scales=xsc[:, lo:lo + P], in_=gx[:, 4 * lo:4 * (lo + P)])
+
+        def sxmm(rt):
+            bank = psT.tile([P, 512], F32, name="sx%d" % rt, tag="T")
+            for g in range(4):
+                nc.tensor.matmul(out=bank[:], lhsT=ones_b[:, 0:P], rhs=gx[:, g * 2048 + rt * 512:g * 2048 + (rt + 1) * 512],
+                                 start=(g == 0), stop=(g == 3))
+            tb[("s", rt)] = bank
+
+        def rsx(rt):
+            nc.vector.tensor_reduce(out=sxr[:, rt * P:(rt + 1) * P], in_=tb[("s", rt)][:].rearrange("p (r t) -> p r t", t=4),
+                                    axis=AX.X, op=ALU.add)
+
+        def tw(b, which=(0, 1, 2, 3)):
+            w32 = wt[b][:].bitcast(F32)
+            for i in which:
+                e, gp = i // 2, i % 2
+                bank = psT.tile([P, 512], F32, name="tw%d_%d" % (b, i), tag="T")
+                four_transposes(bank, w32, [e * 1024 + (2 * gp + gl) * 256 + u for gl in range(2) for u in range(2)])
+                tb[(b, i)] = bank
+
+        def ew(b, i, eng):
+            if i == 0:
+                gw[b] = stage.tile([P, 4096], BF16, name="gw%d" % b, tag="gw", align_bytes=64)
+            dst = gw[b][:].bitcast(F32)[:, i * 512:(i + 1) * 512].rearrange("p (g o u) -> p g o u", g=2, u=2)
+            copy_on(eng, dst, tb[(b, i)][:].rearrange("p (g u o) -> p g o u", g=2, u=2))
+
+        def qw(b, half=None):
+            if half != 1:
+                wc[b] = stage.tile([P, 1024], U32, name="wc%d" % b, tag="wc", align_bytes=64)
+                ws[b] = stage.tile([P, 1024], U8, name="ws%d" % b, tag="ws", align_bytes=64)
+            if half is None:
+                nc.vector.quantize_mx(out=wc[b][:].bitcast(FP8X4), scales=ws[b][:], in_=gw[b][:])
+            else:
+                lo = half * 512
+                nc.vector.quantize_mx(out=wc[b][:, lo:lo + 512].bitcast(FP8X4), scales=ws[b][:, lo:lo + 512], in_=gw[b][:, 4 * lo:4 * lo + 2048])
+
+        def mm(b, es=(0, 1), gs=(0, 1, 2, 3)):
+            rc, rs = (xc, xsc) if b < 8 else (hc, hsc)
+            for e in es:
+                if gs[0] == 0:
+                    mb[(b, e)] = psM.tile([P, 512], F32, name="m%d_%d" % (b, e), tag="M")
+            seq = [(e, g) for e in es for g in gs]
+            for e, g in seq:
+                lo = (e * 4 + g) * P
+                nc.tensor.matmul_mx(out=mb[(b, e)][:], lhsT=wc[b][:, lo:lo + P].bitcast(FP8X4), lhsT_scale=ws[b][:, lo:lo + P],
+                                    rhs=rc[:, g * 512:(g + 1) * 512].bitcast(FP8X4), rhs_scale=rs[:, g * 512:(g + 1) * 512],
+                                    start=(g == 0), stop=(g == 3))
+
+        def msum(b, e):
+            col = (2 * (b % 2) + e) * P + b // 2 if b < 8 else (b - 8) * 2 + e
+            return mp[b // 8][:, col:col + 1]
+
+        def act(b, e):
+            j = (b // 8) * 16 + (b % 8) * 2 + e
+            vt[(b, e)] = work.tile([P, ROWS], F32, name="v%d_%d" % (b, e), tag="v", bufs=NV)
+            nc.scalar.activation(out=vt[(b, e)][:], in_=mb[(b, e)][:], func=ACT.Relu, bias=biasf[:, j:j + 1], scale=1.0,
+                                 accum_out=msum(b, e))
+            if b >= 8:
+                rep[(b, e)] = work.tile([P, P], F32, name="rep%d_%d" % (b, e), tag="rep", bufs=16)
+                if REP_ENG == "G" and b < 14:
+                    nc.gpsimd.tensor_scalar(out=rep[(b, e)][:], in0=ones_f[:], scalar1=msum(b, e), scalar2=1.0 / ROWS, op0=ALU.mult, op1=ALU.mult)
+                else:
+                    nc.vector.tensor_scalar(out=rep[(b, e)][:], in0=ones_f[:], scalar1=msum(b, e), scalar2=1.0 / ROWS, op0=ALU.mult, op1=ALU.mult)
+
+        pending = []
+        added = [0]
+
+        def hh(b, e):
+            g, t = b // 2, 2 * (b % 2) + e
+            if t == 0:
+                hcn[g] = work.tile([P, 2048], BF16, name="hcn%d" % g, tag="hcn")
+            nc.vector.scalar_tensor_tensor(out=hcn[g][:, t * ROWS:(t + 1) * ROWS], in0=sxc[:], scalar=msum(b, e), in1=vt[(b, e)][:],
+                                           op0=ALU.mult, op1=ALU.add)
+            pending.append((b, e))
+
+        def adds(n):
+            for i in range(n):
+                a = added[0]
+                if a < 2:
+                    nc.vector.tensor_tensor(out=acc[a][:], in0=vt[pending[a]][:], in1=vt[pending[a + 2]][:], op=ALU.add)
+                elif a < 14:
+                    nc.vector.tensor_tensor(out=acc[a % 2][:], in0=acc[a % 2][:], in1=vt[pending[a + 2]][:], op=ALU.add)
+                added[0] = min(a + 1, 14)
+
+        def rg(g):
+            gh[g] = work.tile([P, 2048], BF16, name="gh%d" % g, tag="gh", align_bytes=64)
+            nc.vector.tensor_copy(out=gh[g][:].rearrange("p (c i t) -> p c t i", i=4, t=4),
+                                  in_=hcn[g][:].rearrange("p (t c i) -> p c t i", t=4, i=4))
+
+        def qh(g):
+            nc.vector.quantize_mx(out=hc[:, g * 512:(g + 1) * 512].bitcast(FP8X4), scales=hsc[:, g * 512:(g + 1) * 512], in_=gh[g][:])
+
+        def sh_vector():
+            nc.vector.tensor_reduce(out=s1[:], in_=mp[0][:].rearrange("p (t c) -> p t c", t=4)[:, :, 0:4], axis=AX.XY, op=ALU.add)
+            nc.vector.scalar_tensor_tensor(out=accf[:], in0=sxc[:], scalar=s1[:], in1=acc[0][:], op0=ALU.mult, op1=ALU.add)
+            nc.vector.tensor_tensor(out=accf[:], in0=accf[:], in1=acc[1][:], op=ALU.add)
+
+        def sh_rest():
+            bank = psT.tile([P, 512], F32, name="shb", tag="T")
+            for rb in range(4):
+                nc.tensor.matmul(out=bank[:, rb * 32:(rb + 1) * 32], lhsT=accf[:, rb * P:(rb + 1) * P], rhs=ones_f[:, 0:32], start=True, stop=True)
+            nc.scalar.mul(out=shc[:], in_=bank[:, 0:P].rearrange("p (b n) -> p b n", n=32)[:, :, 0], mul=C)
+
+        def to(b):
+            for k in range(2):
+                bank = psT.tile([P, 512], F32, name="to%d_%d" % (b, k), tag="T")
+                for l in range(2):
+                    for e in range(2):
+                        rb = 2 * k + l
+                        nc.tensor.transpose(out=bank[:, (l * 2 + e) * P:(l * 2 + e + 1) * P], in_=vt[(b, e)][:, rb * P:(rb + 1) * P],
+                                            identity=ident[:])
+                tb[("o", b, k)] = bank
+            bank = psT.tile([P, 512], F32, name="tr%d" % b, tag="T")
+            for e in range(2):
+                nc.tensor.transpose(out=bank[:, e * P:(e + 1) * P], in_=rep[(b, e)][:], identity=ident[:])
+            tb[("r", b)] = bank
+
+        def em(b):
+            c = b - 8
+            nc.scalar.copy(out=m2b[:, c * 256:(c + 1) * 256].rearrange("r (p e) -> r p e", e=2),
+                           in_=tb[("r", b)][:, 0:256].rearrange("r (e p) -> r p e", e=2))
+
+        def eo(b):
+            c = b - 8
+            ob[b] = work.tile([P, 1024], F32, name="o%d" % b, tag="o", bufs=3)
+            for rb in range(4):
+                k, l = rb // 2, rb % 2
+                nc.vector.scalar_tensor_tensor(out=ob[b][:, rb * 256:(rb + 1) * 256].rearrange("r (p e) -> r p e", e=2),
+                                               in0=m2b[:, c * 256:(c + 1) * 256].rearrange("r (p e) -> r p e", e=2),
+                                               scalar=shc[:, rb:rb + 1],
+                                               in1=tb[("o", b, k)][:, l * 256:(l + 1) * 256].rearrange("r (e p) -> r p e", e=2),
+                                               op0=ALU.mult, op1=ALU.add)
+                if b == 15 and rb % 2 == 1:
+                    nc.sync.dma_start(out=out_0.rearrange("(k r) o -> r k o", r=P)[:, rb - 1:rb + 1, c * 256:(c + 1) * 256],
+                                      in_=ob[b][:].rearrange("r (k o) -> r k o", k=4)[:, rb - 1:rb + 1, :])
+            if b < 15:
+                nc.sync.dma_start(out=out_0.rearrange("(k r) o -> r k o", r=P)[:, :, c * 256:(c + 1) * 256],
+                                  in_=ob[b][:].rearrange("r (k o) -> r k o", k=4))
+
+        def mout1():
+            bank = psT.tile([P, 512], F32, name="mo", tag="T")
+            for t in range(4):
+                nc.tensor.transpose(out=bank[:, t * P:(t + 1) * P], in_=mp[0][:, t * P:(t + 1) * P], identity=ident[:])
+            ms = work.tile([P, 512], F32, name="ms", tag="ms", bufs=1)
+            nc.scalar.activation(out=ms[:].rearrange("c (p t) -> c p t", t=4), in_=bank[:].rearrange("c (t p) -> c p t", t=4),
+                                 func=ACT.Copy, scale=1.0 / ROWS)
+            nc.sync.dma_start(out=out_1.rearrange("(g n) -> g n", n=512), in_=ms[0:4, :])
+
+        wt[0] = w0
+        for b in range(1, NW - 2):
+            load(b)
+
+        def txe(rt, engines):
+            tx(rt)
+            ex(rt, 0, engines[0])
+            ex(rt, 1, engines[1])
+
+        txe(0, "VS")
+        warm_up(WARM1)
+        bank = psT.tile([P, 512], F32, name="tbias", tag="T")
+        for h in range(2):
+            nc.tensor.transpose(out=bank[:, h * P:(h + 1) * P], in_=bz[:].bitcast(F32)[:, h:h + 255:2], identity=ident[:])
+        nc.tensor.transpose(out=bank[:, 2 * P:3 * P], in_=bz[:].bitcast(F32)[:, 0:P], identity=ident[:])
+        nc.vector.tensor_copy(out=bw[:, 0:8].rearrange("p (g h) -> p g h", h=2), in_=bank[:, 0:2 * P].rearrange("p (h c) -> p c h", h=2)[:, 0:4, :])
+        nc.vector.tensor_copy(out=bw[:, 8:16], in_=bank[:, 2 * P + 4:2 * P + 12])
+        nc.vector.tensor_copy(out=biasf[:], in_=bw[:].bitcast(BF16))
+        qx(0)
+        txe(1, "VS")
+        load(NW - 2)
+        sxmm(0)
+        rsx(0)
+        qx(1)
+        txe(2, "VS")
+        tw(0, (0, 1))
+        ew(0, 0, "S")
+        ew(0, 1, "V")
+        qx(2)
+        qw(0, 0)
+        txe(3, "SV")
+        load(NW - 1)
+        qx(3)
+        sxmm(1)
+        tw(0, (2, 3))
+        load(NW)
+        ew(0, 2, "S")
+        ew(0, 3, "V")
+        rsx(1)
+        qw(0, 1)
+
+        sh_step = [99]
+        twd = [0]
+        turned = [8]
+        def turn_next(b):
+            if b >= sh_step[0] + SH_DELAY and turned[0] <= min(15, b - (LAG if b < 14 else 1)):
+                to(turned[0])
+                em(turned[0])
+                if turned[0] == 15:
+                    nc.sync.dma_start(out=out_2.rearrange("(a n) -> a n", a=1), in_=m2b[0:1, :])
+                eo(turned[0])
+                turned[0] = turned[0] + 1
+
+        for b in range(20):
+            prev = b - 1
+            tlist = [t for t in range(twd[0] + 1, min(15, b + AH[min(b, 9)]) + 1)]
+            if b == 0:
+                mm(0, (0,))
+            for t in tlist:
+                tw(t)
+                twd[0] = t
+                if t + NW <= 15:
+                    load(t + NW)
+                if t != tlist[-1]:
+                    for i in range(4):
+                        ew(t, i, "SVSV"[i])
+            if 0 <= prev <= 15:
+                act(prev, 1)
+                if prev <= 7:
+                    hh(prev, 1)
+                    if prev % 2 == 1:
+                        rg(prev // 2)
+                    if prev == 7:
+                        qh(3)
+            if len(tlist) > 0:
+                for i in range(4):
+                    ew(tlist[-1], i, EW_ENG[tlist[-1] // 8][i])
+            if b == sh_step[0] + SH_DELAY:
+                sh_rest()
+            for i in range(TO_PER_STEP):
+                turn_next(b)
+            if b == 9:
+                mout1()
+            if b == 0:
+                act(0, 0)
+                mm(0, (1,))
+                sxmm(2)
+                sxmm(3)
+            elif b == 8:
+                mm(8, (0, 1), (0, 1, 2))
+                tx_ = twd[0] + 1
+                tw(tx_)
+                twd[0] = tx_
+                if tx_ + NW <= 15:
+                    load(tx_ + NW)
+                for i in range(4):
+                    ew(tx_, i, "SSSS"[i])
+                tlist.append(tx_)
+                mm(8, (0, 1), (3,))
+                act(8, 0)
+            elif b <= 15:
+                mm(b)
+                act(b, 0)
+            for t in tlist:
+                qw(t)
+                if b == 8 and t == 9:
+                    adds(ADDS_8)
+            if prev % 2 == 1 and 0 < prev < 7:
+                qh(prev // 2)
+            if b == 0:
+                rsx(2)
+                rsx(3)
+                nc.vector.tensor_scalar(out=sxc[:], in0=sxr[:], scalar1=C / ROWS, scalar2=None, op0=ALU.mult)
+            if b <= 7:
+                hh(b, 0)
+            if b >= 8 and sh_step[0] == 99:
+                adds(ADDS_L2)
+                if added[0] == 14:
+                    sh_vector()
+                    sh_step[0] = b

@@ -18,18 +18,19 @@ C = 0.01 * 0.001 / 1
 FLOPS = 2 * 2 * 512 * 2048 * 2048
 
 NW = 6
-EW_ENG = ["SSSS", "SSSS"]
-EW0_ENG = "SVSV"
-ADDS_L2 = 5
-ADDS_8 = 3
-LAG = 2
-TO_PER_STEP = 2
-SH_DELAY = 3
-REP_ENG = "G"
-NV = 18
+NV = 17
+NPW = 2
 WARM0 = 4
 WARM1 = 2
-AH = [1, 1, 1, 1, 1, 1, 1, 1, 1, 2]
+PERM = {(b, e): "V" for b in range(3, 16) for e in range(2) if b not in (7, 8) and (e == 0 or b not in (4, 9, 10, 11))}
+ADD = [0] * 8 + [3] * 5 + [0] * 7
+AHEAD = [1] * 8 + [2] * 12
+SX = "VVVP"
+HX = ["VS", "SV", "SS", "SS"]
+HW = "SSSS"
+TPOS = 1
+TPS = 2
+EWE = ["SSSS"] * 16
 
 
 def tile_optimalnet_pa_kernel(tc, x, W1, b1, W2, b2, out_0, out_1, out_2):
@@ -95,6 +96,7 @@ def tile_optimalnet_pa_kernel(tc, x, W1, b1, W2, b2, out_0, out_1, out_2):
         bw = const.tile([P, 16], F32, name="bw")
         biasf = const.tile([P, 32], F32, name="biasf")
         sxr = const.tile([P, ROWS], F32, name="sxr")
+        sxp = const.tile([P, 4], F32, name="sxp")
         sxc = const.tile([P, ROWS], F32, name="sxc")
         acc = [const.tile([P, ROWS], F32, name="acc0"), const.tile([P, ROWS], F32, name="acc1")]
         accf = const.tile([P, ROWS], F32, name="accf")
@@ -104,22 +106,23 @@ def tile_optimalnet_pa_kernel(tc, x, W1, b1, W2, b2, out_0, out_1, out_2):
 
         w1src = W1.rearrange("(g p h e) k -> g h p (e k)", p=P, h=2, e=2)
         w2src = W2.rearrange("(c p e) k -> c p (e k)", p=P, e=2)
-        wt, tb, gw, wc, ws, mb, vt, ob, hcn, gh, rep = {}, {}, {}, {}, {}, {}, {}, {}, {}, {}, {}
+        pw, wt, tb, gw, wc, ws, mb, vt, ob, hcn, gh = {}, {}, {}, {}, {}, {}, {}, {}, {}, {}, {}
 
         def load(b):
-            t = win.tile([P, 4096], BF16, name="w%d" % b, tag="w")
-            nc.sync.dma_start(out=t[:], in_=w1src[b // 2][b % 2] if b < 8 else w2src[b - 8])
-            wt[b] = t
+            if b <= 15:
+                t = win.tile([P, 4096], BF16, name="w%d" % b, tag="w")
+                nc.sync.dma_start(out=t[:], in_=w1src[b // 2][b % 2] if b < 8 else w2src[b - 8])
+                wt[b] = t
 
-        def four_transposes(bank, src32, cols):
+        def four_transposes(bank, src32, cols, step):
             for i in range(4):
-                nc.tensor.transpose(out=bank[:, i * P:(i + 1) * P], in_=src32[:, cols[i]:cols[i] + 255:2], identity=ident[:])
+                nc.tensor.transpose(out=bank[:, i * P:(i + 1) * P], in_=src32[:, cols[i]:cols[i] + step * P - step + 1:step], identity=ident[:])
 
         def tx(rt):
             x32 = xt[rt // 2][:].bitcast(F32)
             for gp in range(2):
                 bank = psT.tile([P, 512], F32, name="tx%d_%d" % (rt, gp), tag="T")
-                four_transposes(bank, x32, [(rt % 2) * 1024 + (2 * gp + gl) * 256 + u for gl in range(2) for u in range(2)])
+                four_transposes(bank, x32, [(rt % 2) * 1024 + (2 * gp + gl) * 256 + u for gl in range(2) for u in range(2)], 2)
                 tb[("x", rt, gp)] = bank
 
         def ex(rt, gp, eng):
@@ -131,23 +134,48 @@ def tile_optimalnet_pa_kernel(tc, x, W1, b1, W2, b2, out_0, out_1, out_2):
                 lo = g * 512 + rt * P
                 nc.vector.quantize_mx(out=xc[:, lo:lo + P].bitcast(FP8X4), scales=xsc[:, lo:lo + P], in_=gx[:, 4 * lo:4 * (lo + P)])
 
-        def sxmm(rt):
-            bank = psT.tile([P, 512], F32, name="sx%d" % rt, tag="T")
-            for g in range(4):
-                nc.tensor.matmul(out=bank[:], lhsT=ones_b[:, 0:P], rhs=gx[:, g * 2048 + rt * 512:g * 2048 + (rt + 1) * 512],
-                                 start=(g == 0), stop=(g == 3))
-            tb[("s", rt)] = bank
+        def sx(rt):
+            if SX[rt] == "P":
+                bank = psT.tile([P, 512], F32, name="sx%d" % rt, tag="T")
+                for g in range(4):
+                    nc.tensor.matmul(out=bank[:], lhsT=ones_b[:, 0:P], rhs=gx[:, g * 2048 + rt * 512:g * 2048 + (rt + 1) * 512],
+                                     start=(g == 0), stop=(g == 3))
+                nc.vector.tensor_reduce(out=sxr[:, rt * P:(rt + 1) * P], in_=bank[:].rearrange("p (r t) -> p r t", t=4),
+                                        axis=AX.X, op=ALU.add)
+            else:
+                junk = stage.tile([P, 2048], BF16, name="jk%d" % rt, tag="jk", bufs=1)
+                nc.vector.tensor_scalar(out=junk[:], in0=xt[rt // 2][:, (rt % 2) * 2048:(rt % 2) * 2048 + 2048], scalar1=1.0, scalar2=0.0,
+                                        op0=ALU.mult, op1=ALU.add, accum_out=sxp[:, rt:rt + 1])
 
-        def rsx(rt):
-            nc.vector.tensor_reduce(out=sxr[:, rt * P:(rt + 1) * P], in_=tb[("s", rt)][:].rearrange("p (r t) -> p r t", t=4),
-                                    axis=AX.X, op=ALU.add)
+        def sx_spread():
+            rts = [rt for rt in range(4) if SX[rt] != "P"]
+            if len(rts) > 0:
+                lo, hi = rts[0] * P, (rts[-1] + 1) * P
+                bank = psT.tile([P, 512], F32, name="sxb", tag="T")
+                for rt in rts:
+                    nc.tensor.transpose(out=bank[:, rt * P:(rt + 1) * P], in_=sxp[:, rt:rt + 1].to_broadcast([P, P]), identity=ident[:])
+                nc.scalar.mul(out=sxc[:, lo:hi], in_=bank[:, lo:hi], mul=C / ROWS)
+            for rt in range(4):
+                if SX[rt] == "P":
+                    nc.vector.tensor_scalar(out=sxc[:, rt * P:(rt + 1) * P], in0=sxr[:, rt * P:(rt + 1) * P], scalar1=C / ROWS, scalar2=None, op0=ALU.mult)
+
+        def perm(b, es=(0, 1)):
+            for e in es:
+                if (b, e) in PERM:
+                    if b not in pw:
+                        pw[b] = stage.tile([P, 2048], F32, name="pw%d" % b, tag="pw", bufs=NPW)
+                    copy_on(PERM[(b, e)], pw[b][:, e * 1024:(e + 1) * 1024].rearrange("p (g u w) -> p g u w", g=4, u=2),
+                            wt[b][:, e * 2048:(e + 1) * 2048].bitcast(F32).rearrange("p (g w u) -> p g u w", g=4, u=2))
 
         def tw(b, which=(0, 1, 2, 3)):
             w32 = wt[b][:].bitcast(F32)
             for i in which:
                 e, gp = i // 2, i % 2
                 bank = psT.tile([P, 512], F32, name="tw%d_%d" % (b, i), tag="T")
-                four_transposes(bank, w32, [e * 1024 + (2 * gp + gl) * 256 + u for gl in range(2) for u in range(2)])
+                if (b, e) in PERM:
+                    four_transposes(bank, pw[b], [e * 1024 + (2 * gp + gl) * 256 + u * P for gl in range(2) for u in range(2)], 1)
+                else:
+                    four_transposes(bank, w32, [e * 1024 + (2 * gp + gl) * 256 + u for gl in range(2) for u in range(2)], 2)
                 tb[(b, i)] = bank
 
         def ew(b, i, eng):
@@ -171,12 +199,11 @@ def tile_optimalnet_pa_kernel(tc, x, W1, b1, W2, b2, out_0, out_1, out_2):
             for e in es:
                 if gs[0] == 0:
                     mb[(b, e)] = psM.tile([P, 512], F32, name="m%d_%d" % (b, e), tag="M")
-            seq = [(e, g) for e in es for g in gs]
-            for e, g in seq:
-                lo = (e * 4 + g) * P
-                nc.tensor.matmul_mx(out=mb[(b, e)][:], lhsT=wc[b][:, lo:lo + P].bitcast(FP8X4), lhsT_scale=ws[b][:, lo:lo + P],
-                                    rhs=rc[:, g * 512:(g + 1) * 512].bitcast(FP8X4), rhs_scale=rs[:, g * 512:(g + 1) * 512],
-                                    start=(g == 0), stop=(g == 3))
+                for g in gs:
+                    lo = (e * 4 + g) * P
+                    nc.tensor.matmul_mx(out=mb[(b, e)][:], lhsT=wc[b][:, lo:lo + P].bitcast(FP8X4), lhsT_scale=ws[b][:, lo:lo + P],
+                                        rhs=rc[:, g * 512:(g + 1) * 512].bitcast(FP8X4), rhs_scale=rs[:, g * 512:(g + 1) * 512],
+                                        start=(g == 0), stop=(g == 3))
 
         def msum(b, e):
             col = (2 * (b % 2) + e) * P + b // 2 if b < 8 else (b - 8) * 2 + e
@@ -187,12 +214,6 @@ def tile_optimalnet_pa_kernel(tc, x, W1, b1, W2, b2, out_0, out_1, out_2):
             vt[(b, e)] = work.tile([P, ROWS], F32, name="v%d_%d" % (b, e), tag="v", bufs=NV)
             nc.scalar.activation(out=vt[(b, e)][:], in_=mb[(b, e)][:], func=ACT.Relu, bias=biasf[:, j:j + 1], scale=1.0,
                                  accum_out=msum(b, e))
-            if b >= 8:
-                rep[(b, e)] = work.tile([P, P], F32, name="rep%d_%d" % (b, e), tag="rep", bufs=16)
-                if REP_ENG == "G" and b < 14:
-                    nc.gpsimd.tensor_scalar(out=rep[(b, e)][:], in0=ones_f[:], scalar1=msum(b, e), scalar2=1.0 / ROWS, op0=ALU.mult, op1=ALU.mult)
-                else:
-                    nc.vector.tensor_scalar(out=rep[(b, e)][:], in0=ones_f[:], scalar1=msum(b, e), scalar2=1.0 / ROWS, op0=ALU.mult, op1=ALU.mult)
 
         pending = []
         added = [0]
@@ -208,11 +229,10 @@ def tile_optimalnet_pa_kernel(tc, x, W1, b1, W2, b2, out_0, out_1, out_2):
         def adds(n):
             for i in range(n):
                 a = added[0]
-                if a < 2:
-                    nc.vector.tensor_tensor(out=acc[a][:], in0=vt[pending[a]][:], in1=vt[pending[a + 2]][:], op=ALU.add)
-                elif a < 14:
-                    nc.vector.tensor_tensor(out=acc[a % 2][:], in0=acc[a % 2][:], in1=vt[pending[a + 2]][:], op=ALU.add)
-                added[0] = min(a + 1, 14)
+                if a < 14 and a + 2 < len(pending):
+                    first = vt[pending[a]] if a < 2 else acc[a % 2]
+                    nc.vector.tensor_tensor(out=acc[a % 2][:], in0=first[:], in1=vt[pending[a + 2]][:], op=ALU.add)
+                    added[0] = a + 1
 
         def rg(g):
             gh[g] = work.tile([P, 2048], BF16, name="gh%d" % g, tag="gh", align_bytes=64)
@@ -244,13 +264,13 @@ def tile_optimalnet_pa_kernel(tc, x, W1, b1, W2, b2, out_0, out_1, out_2):
                 tb[("o", b, k)] = bank
             bank = psT.tile([P, 512], F32, name="tr%d" % b, tag="T")
             for e in range(2):
-                nc.tensor.transpose(out=bank[:, e * P:(e + 1) * P], in_=rep[(b, e)][:], identity=ident[:])
+                nc.tensor.transpose(out=bank[:, e * P:(e + 1) * P], in_=msum(b, e).to_broadcast([P, P]), identity=ident[:])
             tb[("r", b)] = bank
 
         def em(b):
             c = b - 8
-            nc.scalar.copy(out=m2b[:, c * 256:(c + 1) * 256].rearrange("r (p e) -> r p e", e=2),
-                           in_=tb[("r", b)][:, 0:256].rearrange("r (e p) -> r p e", e=2))
+            nc.scalar.mul(out=m2b[:, c * 256:(c + 1) * 256].rearrange("r (p e) -> r p e", e=2),
+                          in_=tb[("r", b)][:, 0:256].rearrange("r (e p) -> r p e", e=2), mul=1.0 / ROWS)
 
         def eo(b):
             c = b - 8
@@ -287,7 +307,7 @@ def tile_optimalnet_pa_kernel(tc, x, W1, b1, W2, b2, out_0, out_1, out_2):
             ex(rt, 0, engines[0])
             ex(rt, 1, engines[1])
 
-        txe(0, "VS")
+        txe(0, HX[0])
         warm_up(WARM1)
         bank = psT.tile([P, 512], F32, name="tbias", tag="T")
         for h in range(2):
@@ -296,105 +316,110 @@ def tile_optimalnet_pa_kernel(tc, x, W1, b1, W2, b2, out_0, out_1, out_2):
         nc.vector.tensor_copy(out=bw[:, 0:8].rearrange("p (g h) -> p g h", h=2), in_=bank[:, 0:2 * P].rearrange("p (h c) -> p c h", h=2)[:, 0:4, :])
         nc.vector.tensor_copy(out=bw[:, 8:16], in_=bank[:, 2 * P + 4:2 * P + 12])
         nc.vector.tensor_copy(out=biasf[:], in_=bw[:].bitcast(BF16))
+        sx(0)
         qx(0)
-        txe(1, "VS")
+        txe(1, HX[1])
+        sx(1)
         load(NW - 2)
-        sxmm(0)
-        rsx(0)
         qx(1)
-        txe(2, "VS")
+        txe(2, HX[2])
+        perm(0, (0,))
         tw(0, (0, 1))
-        ew(0, 0, "S")
-        ew(0, 1, "V")
+        ew(0, 0, HW[0])
+        ew(0, 1, HW[1])
+        sx(2)
         qx(2)
+        txe(3, HX[3])
         qw(0, 0)
-        txe(3, "SV")
-        load(NW - 1)
-        qx(3)
-        sxmm(1)
+        perm(0, (1,))
         tw(0, (2, 3))
+        qx(3)
+        ew(0, 2, HW[2])
+        ew(0, 3, HW[3])
+        sx(3)
+        load(NW - 1)
         load(NW)
-        ew(0, 2, "S")
-        ew(0, 3, "V")
-        rsx(1)
         qw(0, 1)
+        perm(1)
+        perm(2)
 
-        sh_step = [99]
-        twd = [0]
+        done_t, done_q, done_p = 0, 0, 2
+        sh_step = 99
         turned = [8]
-        def turn_next(b):
-            if b >= sh_step[0] + SH_DELAY and turned[0] <= min(15, b - (LAG if b < 14 else 1)):
-                to(turned[0])
-                em(turned[0])
-                if turned[0] == 15:
-                    nc.sync.dma_start(out=out_2.rearrange("(a n) -> a n", a=1), in_=m2b[0:1, :])
-                eo(turned[0])
-                turned[0] = turned[0] + 1
+        b = 0
 
-        for b in range(20):
+        def turn_some():
+            for i in range(TPS):
+                if b > sh_step - TPOS + 1 and turned[0] <= min(15, b - 1):
+                    to(turned[0])
+                    em(turned[0])
+                    if turned[0] == 15:
+                        nc.sync.dma_start(out=out_2.rearrange("(a n) -> a n", a=1), in_=m2b[0:1, :])
+                    eo(turned[0])
+                    turned[0] = turned[0] + 1
+
+        while turned[0] <= 15:
             prev = b - 1
-            tlist = [t for t in range(twd[0] + 1, min(15, b + AH[min(b, 9)]) + 1)]
-            if b == 0:
-                mm(0, (0,))
-            for t in tlist:
-                tw(t)
-                twd[0] = t
-                if t + NW <= 15:
-                    load(t + NW)
-                if t != tlist[-1]:
-                    for i in range(4):
-                        ew(t, i, "SVSV"[i])
+            ahead = min(15, b + AHEAD[min(b, 19)])
+            t_list = list(range(done_t + 1, ahead + 1))
             if 0 <= prev <= 15:
                 act(prev, 1)
-                if prev <= 7:
-                    hh(prev, 1)
-                    if prev % 2 == 1:
-                        rg(prev // 2)
-                    if prev == 7:
-                        qh(3)
-            if len(tlist) > 0:
+            if 0 <= prev <= 7:
+                hh(prev, 1)
+                if prev % 2 == 1:
+                    rg(prev // 2)
+            if b == 8:
+                qh(3)
+            for t in range(done_q + 1, done_t + 1):
+                qw(t)
+                done_q = t
+            if len(t_list) > 0:
+                t = t_list[0]
+                tw(t)
+                load(t + NW)
+                done_t = t
                 for i in range(4):
-                    ew(tlist[-1], i, EW_ENG[tlist[-1] // 8][i])
-            if b == sh_step[0] + SH_DELAY:
-                sh_rest()
-            for i in range(TO_PER_STEP):
-                turn_next(b)
+                    ew(t, i, EWE[t][i])
+            need_p = min(15, max(ahead, b + 1 + AHEAD[min(b + 1, 19)]))
+            for t in range(done_p + 1, need_p + 1):
+                perm(t)
+                done_p = t
+            if prev % 2 == 1 and 0 < prev < 7:
+                qh(prev // 2)
+            if TPOS == 0:
+                turn_some()
             if b == 9:
                 mout1()
             if b == 0:
+                mm(0, (0,))
                 act(0, 0)
                 mm(0, (1,))
-                sxmm(2)
-                sxmm(3)
+                sx_spread()
             elif b == 8:
                 mm(8, (0, 1), (0, 1, 2))
-                tx_ = twd[0] + 1
-                tw(tx_)
-                twd[0] = tx_
-                if tx_ + NW <= 15:
-                    load(tx_ + NW)
-                for i in range(4):
-                    ew(tx_, i, "SSSS"[i])
-                tlist.append(tx_)
+                for t in t_list[1:]:
+                    tw(t)
+                    load(t + NW)
+                    done_t = t
+                    for i in range(4):
+                        ew(t, i, EWE[t][i])
                 mm(8, (0, 1), (3,))
                 act(8, 0)
             elif b <= 15:
                 mm(b)
                 act(b, 0)
-            for t in tlist:
-                qw(t)
-                if b == 8 and t == 9:
-                    adds(ADDS_8)
-            if prev % 2 == 1 and 0 < prev < 7:
-                qh(prev // 2)
-            if b == 0:
-                rsx(2)
-                rsx(3)
-                nc.vector.tensor_scalar(out=sxc[:], in0=sxr[:], scalar1=C / ROWS, scalar2=None, op0=ALU.mult)
+            if b == sh_step + 1:
+                sh_rest()
+            if TPOS == 1:
+                turn_some()
+            if b + 1 <= 15 and done_q < b + 1:
+                qw(b + 1)
+                done_q = b + 1
             if b <= 7:
                 hh(b, 0)
-            if b >= 8 and sh_step[0] == 99:
-                adds(ADDS_L2)
+            if sh_step == 99:
+                adds(ADD[b])
                 if added[0] == 14:
                     sh_vector()
-                    sh_step[0] = b
+                    sh_step = b
+            b = b + 1

@@ -22,7 +22,7 @@ NV = 17
 NPW = 2
 WARM0 = 4
 WARM1 = 2
-PERM = {(b, e): "V" for b in range(3, 16) for e in range(2) if b not in (7, 8) and (e == 0 or b not in (4, 9, 10, 11))}
+PERM = {}
 ADD = [0] * 8 + [3] * 5 + [0] * 7
 AHEAD = [1] * 8 + [2] * 12
 SX = "VVVP"

@@ -22,15 +22,21 @@ NV = 17
 NPW = 2
 WARM0 = 4
 WARM1 = 2
-PERM = {}
-ADD = [0] * 8 + [3] * 5 + [0] * 7
+L1PAIR = False
+PERM = {(b, e): "V" for b in range(8, 16) for e in range(2)}
+XP = "VVVV"
+ADD = [0] * 5 + [1, 1, 1, 2, 3, 3, 3] + [0] * 8
 AHEAD = [1] * 8 + [2] * 12
-SX = "VVVP"
+SX = "VVVV"
 HX = ["VS", "SV", "SS", "SS"]
 HW = "SSSS"
-TPOS = 1
+TPOS = 2
+SHL = 1
 TPS = 2
 EWE = ["SSSS"] * 16
+REPG = 14
+DN = 128
+DW = 3
 
 
 def tile_optimalnet_pa_kernel(tc, x, W1, b1, W2, b2, out_0, out_1, out_2):
@@ -57,7 +63,7 @@ def tile_optimalnet_pa_kernel(tc, x, W1, b1, W2, b2, out_0, out_1, out_2):
             nc.sync.dma_start(out=xt[rt // 2][:, (rt % 2) * 2048 + lo:(rt % 2) * 2048 + hi], in_=x[rt * P:(rt + 1) * P, lo:hi])
 
         def load_w0(e):
-            nc.sync.dma_start(out=w0[:, e * 2048:(e + 1) * 2048], in_=W1.rearrange("(g p h e) k -> g h p e k", p=P, h=2, e=2)[0][0][:, e, :])
+            nc.sync.dma_start(out=w0[:].rearrange("p (i k) -> p i k", i=2)[:, :, e * 1024:(e + 1) * 1024], in_=W1.rearrange("(g p i e) k -> g e p i k", p=P, i=2, e=2)[0][0][:, :, e * 1024:(e + 1) * 1024])
 
         load_x(0, 0, 1024)
         load_x(0, 1024, 2048)
@@ -74,17 +80,19 @@ def tile_optimalnet_pa_kernel(tc, x, W1, b1, W2, b2, out_0, out_1, out_2):
         load_w0(1)
         ident = const.tile([P, P], F32, name="ident")
         make_identity(nc, ident[:])
+        identp = const.tile([P, P], F32, name="identp")
+        nc.gpsimd.tensor_copy(out=identp[:].rearrange("p (u j) -> p u j", u=2), in_=ident[:].rearrange("p (j u) -> p u j", u=2))
         ones_f = const.tile([P, P], F32, name="ones_f")
         nc.vector.memset(ones_f[:], 1.0)
         mp = [const.tile([P, 512], F32, name="mp0"), const.tile([P, 16], F32, name="mp1")]
         nc.vector.memset(mp[0][:], 0.0)
         tabl = const.tile([P, 1], F32, name="tabl")
         nc.scalar.activation(out=tabl[:], in_=ones_f[:, 0:1], func=ACT.Relu)
-        warm = psT.tile([P, 512], F32, name="warm", tag="T")
+        warm = psM.tile([P, 512], F32, name="warm", tag="M")
 
-        def warm_up(n):
+        def warm_up(n, cols=512):
             for i in range(n):
-                nc.tensor.matmul(out=warm[:], lhsT=ones_b[:, 0:P], rhs=ones_b[:], start=True, stop=True)
+                nc.tensor.matmul(out=warm[:, 0:cols], lhsT=ones_b[:, 0:P], rhs=ones_b[:, 0:cols], start=True, stop=True)
 
         warm_up(WARM0)
 
@@ -104,25 +112,42 @@ def tile_optimalnet_pa_kernel(tc, x, W1, b1, W2, b2, out_0, out_1, out_2):
         s1 = const.tile([P, 1], F32, name="s1")
         m2b = const.tile([P, 2048], F32, name="m2b")
 
-        w1src = W1.rearrange("(g p h e) k -> g h p (e k)", p=P, h=2, e=2)
+        w1src = W1.rearrange("(g p i e) k -> g e p i k", p=P, i=2, e=2)
         w2src = W2.rearrange("(c p e) k -> c p (e k)", p=P, e=2)
-        pw, wt, tb, gw, wc, ws, mb, vt, ob, hcn, gh = {}, {}, {}, {}, {}, {}, {}, {}, {}, {}, {}
+        pw, wt, tb, gw, wc, ws, mb, vt, ob, hcn, gh, rep = {}, {}, {}, {}, {}, {}, {}, {}, {}, {}, {}, {}
 
         def load(b):
             if b <= 15:
                 t = win.tile([P, 4096], BF16, name="w%d" % b, tag="w")
-                nc.sync.dma_start(out=t[:], in_=w1src[b // 2][b % 2] if b < 8 else w2src[b - 8])
+                if b < 8:
+                    nc.sync.dma_start(out=t[:].rearrange("p (i k) -> p i k", i=2), in_=w1src[b // 2][b % 2])
+                else:
+                    nc.sync.dma_start(out=t[:], in_=w2src[b - 8])
                 wt[b] = t
 
-        def four_transposes(bank, src32, cols, step):
+        def four_transposes(bank, src32, cols, step, idn):
             for i in range(4):
-                nc.tensor.transpose(out=bank[:, i * P:(i + 1) * P], in_=src32[:, cols[i]:cols[i] + step * P - step + 1:step], identity=ident[:])
+                nc.tensor.transpose(out=bank[:, i * P:(i + 1) * P], in_=src32[:, cols[i]:cols[i] + step * P - step + 1:step], identity=idn[:])
+
+        def pairs(eng, out, in_):
+            copy_on(eng, out.rearrange("p (u n i) -> p u n i", u=2, i=2), in_.rearrange("p (n u i) -> p u n i", u=2, i=2))
+
+        pxt = {}
+        sxrep = {}
+
+        def xperm(rt):
+            if L1PAIR:
+                pxt[rt] = stage.tile([P, 1024], F32, name="px%d" % rt, tag="px", bufs=2)
+                pairs(XP[rt], pxt[rt][:], xt[rt // 2][:].bitcast(F32)[:, (rt % 2) * 1024:(rt % 2) * 1024 + 1024])
 
         def tx(rt):
             x32 = xt[rt // 2][:].bitcast(F32)
             for gp in range(2):
                 bank = psT.tile([P, 512], F32, name="tx%d_%d" % (rt, gp), tag="T")
-                four_transposes(bank, x32, [(rt % 2) * 1024 + (2 * gp + gl) * 256 + u for gl in range(2) for u in range(2)], 2)
+                if L1PAIR:
+                    four_transposes(bank, pxt[rt], [u * 512 + (2 * gp + gl) * P for gl in range(2) for u in range(2)], 1, ident)
+                else:
+                    four_transposes(bank, x32, [(rt % 2) * 1024 + (2 * gp + gl) * 256 + u for gl in range(2) for u in range(2)], 2, ident)
                 tb[("x", rt, gp)] = bank
 
         def ex(rt, gp, eng):
@@ -140,12 +165,18 @@ def tile_optimalnet_pa_kernel(tc, x, W1, b1, W2, b2, out_0, out_1, out_2):
                 for g in range(4):
                     nc.tensor.matmul(out=bank[:], lhsT=ones_b[:, 0:P], rhs=gx[:, g * 2048 + rt * 512:g * 2048 + (rt + 1) * 512],
                                      start=(g == 0), stop=(g == 3))
-                nc.vector.tensor_reduce(out=sxr[:, rt * P:(rt + 1) * P], in_=bank[:].rearrange("p (r t) -> p r t", t=4),
-                                        axis=AX.X, op=ALU.add)
+                tb[("s", rt)] = bank
             else:
                 junk = stage.tile([P, 2048], BF16, name="jk%d" % rt, tag="jk", bufs=1)
                 nc.vector.tensor_scalar(out=junk[:], in0=xt[rt // 2][:, (rt % 2) * 2048:(rt % 2) * 2048 + 2048], scalar1=1.0, scalar2=0.0,
                                         op0=ALU.mult, op1=ALU.add, accum_out=sxp[:, rt:rt + 1])
+                sxrep[rt] = work.tile([P, P], F32, name="sxrep%d" % rt, tag="sxrep", bufs=4)
+                nc.gpsimd.tensor_scalar(out=sxrep[rt][:], in0=ones_f[:], scalar1=sxp[:, rt:rt + 1], scalar2=C / ROWS, op0=ALU.mult, op1=ALU.mult)
+
+        def rsx(rt):
+            if SX[rt] == "P":
+                nc.vector.tensor_reduce(out=sxr[:, rt * P:(rt + 1) * P], in_=tb[("s", rt)][:].rearrange("p (r t) -> p r t", t=4),
+                                        axis=AX.X, op=ALU.add)
 
         def sx_spread():
             rts = [rt for rt in range(4) if SX[rt] != "P"]
@@ -153,8 +184,8 @@ def tile_optimalnet_pa_kernel(tc, x, W1, b1, W2, b2, out_0, out_1, out_2):
                 lo, hi = rts[0] * P, (rts[-1] + 1) * P
                 bank = psT.tile([P, 512], F32, name="sxb", tag="T")
                 for rt in rts:
-                    nc.tensor.transpose(out=bank[:, rt * P:(rt + 1) * P], in_=sxp[:, rt:rt + 1].to_broadcast([P, P]), identity=ident[:])
-                nc.scalar.mul(out=sxc[:, lo:hi], in_=bank[:, lo:hi], mul=C / ROWS)
+                    nc.tensor.transpose(out=bank[:, rt * P:(rt + 1) * P], in_=sxrep[rt][:], identity=ident[:])
+                nc.scalar.copy(out=sxc[:, lo:hi], in_=bank[:, lo:hi])
             for rt in range(4):
                 if SX[rt] == "P":
                     nc.vector.tensor_scalar(out=sxc[:, rt * P:(rt + 1) * P], in0=sxr[:, rt * P:(rt + 1) * P], scalar1=C / ROWS, scalar2=None, op0=ALU.mult)
@@ -164,25 +195,35 @@ def tile_optimalnet_pa_kernel(tc, x, W1, b1, W2, b2, out_0, out_1, out_2):
                 if (b, e) in PERM:
                     if b not in pw:
                         pw[b] = stage.tile([P, 2048], F32, name="pw%d" % b, tag="pw", bufs=NPW)
-                    copy_on(PERM[(b, e)], pw[b][:, e * 1024:(e + 1) * 1024].rearrange("p (g u w) -> p g u w", g=4, u=2),
-                            wt[b][:, e * 2048:(e + 1) * 2048].bitcast(F32).rearrange("p (g w u) -> p g u w", g=4, u=2))
+                    if b == 0:
+                        for r in range(2):
+                            copy_on(PERM[(b, e)], pw[b][:, r * 1024:(r + 1) * 1024].rearrange("p (u h n i) -> p h u n i", u=2, h=2, i=2)[:, e],
+                                    wt[b][:, r * 2048 + e * 1024:r * 2048 + (e + 1) * 1024].bitcast(F32).rearrange("p (n u i) -> p u n i", u=2, i=2))
+                    else:
+                        pairs(PERM[(b, e)], pw[b][:, e * 1024:(e + 1) * 1024], wt[b][:, e * 2048:(e + 1) * 2048].bitcast(F32))
 
         def tw(b, which=(0, 1, 2, 3)):
             w32 = wt[b][:].bitcast(F32)
             for i in which:
-                e, gp = i // 2, i % 2
                 bank = psT.tile([P, 512], F32, name="tw%d_%d" % (b, i), tag="T")
-                if (b, e) in PERM:
-                    four_transposes(bank, pw[b], [e * 1024 + (2 * gp + gl) * 256 + u * P for gl in range(2) for u in range(2)], 1)
+                if b < 8:
+                    if L1PAIR:
+                        four_transposes(bank, pw[b], [r * 1024 + u * 512 + i * P for r in range(2) for u in range(2)], 1, identp)
+                    else:
+                        four_transposes(bank, w32, [r * 1024 + i * 256 + u for r in range(2) for u in range(2)], 2, identp)
                 else:
-                    four_transposes(bank, w32, [e * 1024 + (2 * gp + gl) * 256 + u for gl in range(2) for u in range(2)], 2)
+                    e, gp = i // 2, i % 2
+                    four_transposes(bank, pw[b], [e * 1024 + u * 512 + (2 * gp + gl) * P for gl in range(2) for u in range(2)], 1, ident)
                 tb[(b, i)] = bank
 
         def ew(b, i, eng):
             if i == 0:
                 gw[b] = stage.tile([P, 4096], BF16, name="gw%d" % b, tag="gw", align_bytes=64)
-            dst = gw[b][:].bitcast(F32)[:, i * 512:(i + 1) * 512].rearrange("p (g o u) -> p g o u", g=2, u=2)
-            copy_on(eng, dst, tb[(b, i)][:].rearrange("p (g u o) -> p g o u", g=2, u=2))
+            dst = gw[b][:].bitcast(F32)[:, i * 512:(i + 1) * 512]
+            if b < 8:
+                copy_on(eng, dst.rearrange("p (o i u) -> p o i u", i=2, u=2), tb[(b, i)][:].rearrange("p (i u o) -> p o i u", i=2, u=2))
+            else:
+                copy_on(eng, dst.rearrange("p (g o u) -> p g o u", g=2, u=2), tb[(b, i)][:].rearrange("p (g u o) -> p g o u", g=2, u=2))
 
         def qw(b, half=None):
             if half != 1:
@@ -200,26 +241,31 @@ def tile_optimalnet_pa_kernel(tc, x, W1, b1, W2, b2, out_0, out_1, out_2):
                 if gs[0] == 0:
                     mb[(b, e)] = psM.tile([P, 512], F32, name="m%d_%d" % (b, e), tag="M")
                 for g in gs:
-                    lo = (e * 4 + g) * P
+                    lo = (g * 2 + e) * P if b < 8 else (e * 4 + g) * P
                     nc.tensor.matmul_mx(out=mb[(b, e)][:], lhsT=wc[b][:, lo:lo + P].bitcast(FP8X4), lhsT_scale=ws[b][:, lo:lo + P],
                                         rhs=rc[:, g * 512:(g + 1) * 512].bitcast(FP8X4), rhs_scale=rs[:, g * 512:(g + 1) * 512],
                                         start=(g == 0), stop=(g == 3))
 
         def msum(b, e):
-            col = (2 * (b % 2) + e) * P + b // 2 if b < 8 else (b - 8) * 2 + e
+            col = (2 * e + b % 2) * P + b // 2 if b < 8 else (b - 8) * 2 + e
             return mp[b // 8][:, col:col + 1]
 
         def act(b, e):
-            j = (b // 8) * 16 + (b % 8) * 2 + e
+            j = (b // 2 * 2 + e) * 2 + b % 2 if b < 8 else 16 + (b - 8) * 2 + e
             vt[(b, e)] = work.tile([P, ROWS], F32, name="v%d_%d" % (b, e), tag="v", bufs=NV)
             nc.scalar.activation(out=vt[(b, e)][:], in_=mb[(b, e)][:], func=ACT.Relu, bias=biasf[:, j:j + 1], scale=1.0,
                                  accum_out=msum(b, e))
+
+            if b >= 8:
+                rep[(b, e)] = work.tile([P, P], F32, name="rep%d_%d" % (b, e), tag="rep", bufs=6)
+                eng = nc.gpsimd if b < REPG else nc.vector
+                eng.tensor_scalar(out=rep[(b, e)][:], in0=ones_f[:], scalar1=msum(b, e), scalar2=1.0 / ROWS, op0=ALU.mult, op1=ALU.mult)
 
         pending = []
         added = [0]
 
         def hh(b, e):
-            g, t = b // 2, 2 * (b % 2) + e
+            g, t = b // 2, 2 * e + b % 2
             if t == 0:
                 hcn[g] = work.tile([P, 2048], BF16, name="hcn%d" % g, tag="hcn")
             nc.vector.scalar_tensor_tensor(out=hcn[g][:, t * ROWS:(t + 1) * ROWS], in0=sxc[:], scalar=msum(b, e), in1=vt[(b, e)][:],
@@ -254,6 +300,10 @@ def tile_optimalnet_pa_kernel(tc, x, W1, b1, W2, b2, out_0, out_1, out_2):
             nc.scalar.mul(out=shc[:], in_=bank[:, 0:P].rearrange("p (b n) -> p b n", n=32)[:, :, 0], mul=C)
 
         def to(b):
+            bank = psT.tile([P, 512], F32, name="tr%d" % b, tag="T")
+            for e in range(2):
+                nc.tensor.transpose(out=bank[:, e * P:(e + 1) * P], in_=rep[(b, e)][:], identity=ident[:])
+            tb[("r", b)] = bank
             for k in range(2):
                 bank = psT.tile([P, 512], F32, name="to%d_%d" % (b, k), tag="T")
                 for l in range(2):
@@ -262,15 +312,11 @@ def tile_optimalnet_pa_kernel(tc, x, W1, b1, W2, b2, out_0, out_1, out_2):
                         nc.tensor.transpose(out=bank[:, (l * 2 + e) * P:(l * 2 + e + 1) * P], in_=vt[(b, e)][:, rb * P:(rb + 1) * P],
                                             identity=ident[:])
                 tb[("o", b, k)] = bank
-            bank = psT.tile([P, 512], F32, name="tr%d" % b, tag="T")
-            for e in range(2):
-                nc.tensor.transpose(out=bank[:, e * P:(e + 1) * P], in_=msum(b, e).to_broadcast([P, P]), identity=ident[:])
-            tb[("r", b)] = bank
 
         def em(b):
             c = b - 8
-            nc.scalar.mul(out=m2b[:, c * 256:(c + 1) * 256].rearrange("r (p e) -> r p e", e=2),
-                          in_=tb[("r", b)][:, 0:256].rearrange("r (e p) -> r p e", e=2), mul=1.0 / ROWS)
+            nc.scalar.copy(out=m2b[:, c * 256:(c + 1) * 256].rearrange("r (p e) -> r p e", e=2),
+                           in_=tb[("r", b)][:, 0:256].rearrange("r (e p) -> r p e", e=2))
 
         def eo(b):
             c = b - 8
@@ -294,8 +340,9 @@ def tile_optimalnet_pa_kernel(tc, x, W1, b1, W2, b2, out_0, out_1, out_2):
             for t in range(4):
                 nc.tensor.transpose(out=bank[:, t * P:(t + 1) * P], in_=mp[0][:, t * P:(t + 1) * P], identity=ident[:])
             ms = work.tile([P, 512], F32, name="ms", tag="ms", bufs=1)
-            nc.scalar.activation(out=ms[:].rearrange("c (p t) -> c p t", t=4), in_=bank[:].rearrange("c (t p) -> c p t", t=4),
-                                 func=ACT.Copy, scale=1.0 / ROWS)
+            for e in range(2):
+                nc.scalar.activation(out=ms[:].rearrange("c (j u i e) -> c e j u i", u=2, i=2, e=2)[:, e],
+                                     in_=bank[:].rearrange("c (u e j i) -> c e j u i", u=2, e=2, i=2)[:, e], func=ACT.Copy, scale=1.0 / ROWS)
             nc.sync.dma_start(out=out_1.rearrange("(g n) -> g n", n=512), in_=ms[0:4, :])
 
         wt[0] = w0
@@ -307,40 +354,52 @@ def tile_optimalnet_pa_kernel(tc, x, W1, b1, W2, b2, out_0, out_1, out_2):
             ex(rt, 0, engines[0])
             ex(rt, 1, engines[1])
 
+        xperm(0)
         txe(0, HX[0])
         warm_up(WARM1)
+        xperm(1)
         bank = psT.tile([P, 512], F32, name="tbias", tag="T")
+        bzp = const.tile([P, 256], F32, name="bzp")
+        pairs("V", bzp[:], bz[:].bitcast(F32))
         for h in range(2):
-            nc.tensor.transpose(out=bank[:, h * P:(h + 1) * P], in_=bz[:].bitcast(F32)[:, h:h + 255:2], identity=ident[:])
+            nc.tensor.transpose(out=bank[:, h * P:(h + 1) * P], in_=bzp[:, h * P:(h + 1) * P], identity=ident[:])
         nc.tensor.transpose(out=bank[:, 2 * P:3 * P], in_=bz[:].bitcast(F32)[:, 0:P], identity=ident[:])
         nc.vector.tensor_copy(out=bw[:, 0:8].rearrange("p (g h) -> p g h", h=2), in_=bank[:, 0:2 * P].rearrange("p (h c) -> p c h", h=2)[:, 0:4, :])
         nc.vector.tensor_copy(out=bw[:, 8:16], in_=bank[:, 2 * P + 4:2 * P + 12])
         nc.vector.tensor_copy(out=biasf[:], in_=bw[:].bitcast(BF16))
+        txe(1, HX[1])
+        warm_up(1, DN)
         sx(0)
         qx(0)
-        txe(1, HX[1])
+        xperm(2)
+        txe(2, HX[2])
+        warm_up(1, DN)
         sx(1)
         load(NW - 2)
         qx(1)
-        txe(2, HX[2])
         perm(0, (0,))
         tw(0, (0, 1))
+        warm_up(1, DN)
         ew(0, 0, HW[0])
         ew(0, 1, HW[1])
-        sx(2)
+        xperm(3)
         qx(2)
         txe(3, HX[3])
-        qw(0, 0)
+        warm_up(1, DN)
         perm(0, (1,))
+        qw(0, 0)
         tw(0, (2, 3))
-        qx(3)
+        warm_up(1, DN)
         ew(0, 2, HW[2])
         ew(0, 3, HW[3])
+        warm_up(DW)
+        qx(3)
+        perm(1)
+        qw(0, 1)
+        sx(2)
         sx(3)
         load(NW - 1)
         load(NW)
-        qw(0, 1)
-        perm(1)
         perm(2)
 
         done_t, done_q, done_p = 0, 0, 2
@@ -350,7 +409,7 @@ def tile_optimalnet_pa_kernel(tc, x, W1, b1, W2, b2, out_0, out_1, out_2):
 
         def turn_some():
             for i in range(TPS):
-                if b > sh_step - TPOS + 1 and turned[0] <= min(15, b - 1):
+                if b >= sh_step + SHL + (0 if TPOS == 1 else 1) and turned[0] <= min(15, b - 1):
                     to(turned[0])
                     em(turned[0])
                     if turned[0] == 15:
@@ -364,6 +423,13 @@ def tile_optimalnet_pa_kernel(tc, x, W1, b1, W2, b2, out_0, out_1, out_2):
             t_list = list(range(done_t + 1, ahead + 1))
             if 0 <= prev <= 15:
                 act(prev, 1)
+            if TPOS == 2:
+                turn_some()
+            if b == 1:
+                for rt in range(4):
+                    rsx(rt)
+                sx_spread()
+                hh(0, 0)
             if 0 <= prev <= 7:
                 hh(prev, 1)
                 if prev % 2 == 1:
@@ -394,7 +460,7 @@ def tile_optimalnet_pa_kernel(tc, x, W1, b1, W2, b2, out_0, out_1, out_2):
                 mm(0, (0,))
                 act(0, 0)
                 mm(0, (1,))
-                sx_spread()
+                pass
             elif b == 8:
                 mm(8, (0, 1), (0, 1, 2))
                 for t in t_list[1:]:
@@ -408,14 +474,14 @@ def tile_optimalnet_pa_kernel(tc, x, W1, b1, W2, b2, out_0, out_1, out_2):
             elif b <= 15:
                 mm(b)
                 act(b, 0)
-            if b == sh_step + 1:
+            if b == sh_step + SHL:
                 sh_rest()
             if TPOS == 1:
                 turn_some()
             if b + 1 <= 15 and done_q < b + 1:
                 qw(b + 1)
                 done_q = b + 1
-            if b <= 7:
+            if 0 < b <= 7:
                 hh(b, 0)
             if sh_step == 99:
                 adds(ADD[b])

@@ -18,25 +18,29 @@ C = 0.01 * 0.001 / 1
 FLOPS = 2 * 2 * 512 * 2048 * 2048
 
 NW = 6
-NV = 17
+NV = 16
 NPW = 2
 WARM0 = 4
 WARM1 = 2
-L1PAIR = False
-PERM = {(b, e): "V" for b in range(8, 16) for e in range(2)}
+RUNS = []
+XRUNS = []
+PAIRED = [g for g0, n, eng in RUNS for g in range(g0, g0 + n)]
+PERM = {(b, e): "S" if (b, e) in ((9, 1), (10, 0)) else "V" for b in range(8, 16) for e in range(2)}
 XP = "VVVV"
-ADD = [0] * 5 + [1, 1, 1, 2, 3, 3, 3] + [0] * 8
+ADD = [0, 1, 2, 2, 1, 1, 1, 2, 2, 2]
 AHEAD = [1] * 8 + [2] * 12
 SX = "VVVV"
-HX = ["VS", "SV", "SS", "SS"]
+HX = ["SS", "SS", "SS", "SS"]
 HW = "SSSS"
-TPOS = 2
 SHL = 1
-TPS = 2
+TPS = 1
 EWE = ["SSSS"] * 16
 REPG = 14
-DN = 128
-DW = 3
+WA, WB, WC, WD = 2, 1, 1, 1
+SPREAD = 3
+HHN = [0, 0, 0, 4, 3, 3, 2, 2, 2]
+DW = 0
+RB = 10
 
 
 def tile_optimalnet_pa_kernel(tc, x, W1, b1, W2, b2, out_0, out_1, out_2):
@@ -74,10 +78,10 @@ def tile_optimalnet_pa_kernel(tc, x, W1, b1, W2, b2, out_0, out_1, out_2):
         nc.sync.dma_start(out=bz[0:4, :], in_=b1.rearrange("(g n) -> g n", n=512))
         nc.sync.dma_start(out=bz[4:12, 0:256], in_=b2.rearrange("(c n) -> c n", n=256))
         load_x(1)
-        load_x(2)
         load_w0(0)
-        load_x(3)
         load_w0(1)
+        load_x(2)
+        load_x(3)
         ident = const.tile([P, P], F32, name="ident")
         make_identity(nc, ident[:])
         identp = const.tile([P, P], F32, name="identp")
@@ -114,7 +118,8 @@ def tile_optimalnet_pa_kernel(tc, x, W1, b1, W2, b2, out_0, out_1, out_2):
 
         w1src = W1.rearrange("(g p i e) k -> g e p i k", p=P, i=2, e=2)
         w2src = W2.rearrange("(c p e) k -> c p (e k)", p=P, e=2)
-        pw, wt, tb, gw, wc, ws, mb, vt, ob, hcn, gh, rep = {}, {}, {}, {}, {}, {}, {}, {}, {}, {}, {}, {}
+        pending = []
+        pw, ps, wt, tb, gw, wc, ws, mb, vt, ob, hcn, gh, rep = {}, {}, {}, {}, {}, {}, {}, {}, {}, {}, {}, {}, {}
 
         def load(b):
             if b <= 15:
@@ -125,9 +130,9 @@ def tile_optimalnet_pa_kernel(tc, x, W1, b1, W2, b2, out_0, out_1, out_2):
                     nc.sync.dma_start(out=t[:], in_=w2src[b - 8])
                 wt[b] = t
 
-        def four_transposes(bank, src32, cols, step, idn):
+        def four_transposes(bank, srcs, idn):
             for i in range(4):
-                nc.tensor.transpose(out=bank[:, i * P:(i + 1) * P], in_=src32[:, cols[i]:cols[i] + step * P - step + 1:step], identity=idn[:])
+                nc.tensor.transpose(out=bank[:, i * P:(i + 1) * P], in_=srcs[i], identity=idn[:])
 
         def pairs(eng, out, in_):
             copy_on(eng, out.rearrange("p (u n i) -> p u n i", u=2, i=2), in_.rearrange("p (n u i) -> p u n i", u=2, i=2))
@@ -136,18 +141,21 @@ def tile_optimalnet_pa_kernel(tc, x, W1, b1, W2, b2, out_0, out_1, out_2):
         sxrep = {}
 
         def xperm(rt):
-            if L1PAIR:
-                pxt[rt] = stage.tile([P, 1024], F32, name="px%d" % rt, tag="px", bufs=2)
-                pairs(XP[rt], pxt[rt][:], xt[rt // 2][:].bitcast(F32)[:, (rt % 2) * 1024:(rt % 2) * 1024 + 1024])
+            pxt[rt] = {}
+            for g0, n, eng in XRUNS:
+                px = stage.tile([P, n * 256], F32, name="px%d_%d" % (rt, g0), tag="px%d" % g0, bufs=2)
+                lo = (rt % 2) * 1024 + g0 * 256
+                pairs(eng, px[:], xt[rt // 2][:].bitcast(F32)[:, lo:lo + n * 256])
+                for g in range(g0, g0 + n):
+                    for u in range(2):
+                        pxt[rt][(g, u)] = px[:, u * n * P + (g - g0) * P:u * n * P + (g - g0 + 1) * P]
 
         def tx(rt):
             x32 = xt[rt // 2][:].bitcast(F32)
             for gp in range(2):
                 bank = psT.tile([P, 512], F32, name="tx%d_%d" % (rt, gp), tag="T")
-                if L1PAIR:
-                    four_transposes(bank, pxt[rt], [u * 512 + (2 * gp + gl) * P for gl in range(2) for u in range(2)], 1, ident)
-                else:
-                    four_transposes(bank, x32, [(rt % 2) * 1024 + (2 * gp + gl) * 256 + u for gl in range(2) for u in range(2)], 2, ident)
+                four_transposes(bank, [pxt[rt].get((g, u), x32[:, (rt % 2) * 1024 + g * 256 + u:(rt % 2) * 1024 + g * 256 + u + 255:2])
+                                       for g in (2 * gp, 2 * gp + 1) for u in range(2)], ident)
                 tb[("x", rt, gp)] = bank
 
         def ex(rt, gp, eng):
@@ -165,18 +173,17 @@ def tile_optimalnet_pa_kernel(tc, x, W1, b1, W2, b2, out_0, out_1, out_2):
                 for g in range(4):
                     nc.tensor.matmul(out=bank[:], lhsT=ones_b[:, 0:P], rhs=gx[:, g * 2048 + rt * 512:g * 2048 + (rt + 1) * 512],
                                      start=(g == 0), stop=(g == 3))
-                tb[("s", rt)] = bank
+                nc.vector.tensor_reduce(out=sxr[:, rt * P:(rt + 1) * P], in_=bank[:].rearrange("p (r t) -> p r t", t=4),
+                                        axis=AX.X, op=ALU.add)
             else:
-                junk = stage.tile([P, 2048], BF16, name="jk%d" % rt, tag="jk", bufs=1)
-                nc.vector.tensor_scalar(out=junk[:], in0=xt[rt // 2][:, (rt % 2) * 2048:(rt % 2) * 2048 + 2048], scalar1=1.0, scalar2=0.0,
-                                        op0=ALU.mult, op1=ALU.add, accum_out=sxp[:, rt:rt + 1])
+                junk = stage.tile([P, 2048], BF16, name="jk%d" % rt, tag="jk" + SX[rt], bufs=1)
+                src = xt[rt // 2][:, (rt % 2) * 2048:(rt % 2) * 2048 + 2048]
+                if SX[rt] == "V":
+                    nc.vector.tensor_scalar(out=junk[:], in0=src, scalar1=1.0, scalar2=0.0, op0=ALU.mult, op1=ALU.add, accum_out=sxp[:, rt:rt + 1])
+                else:
+                    nc.scalar.activation(out=junk[:], in_=src, func=ACT.Identity, accum_out=sxp[:, rt:rt + 1])
                 sxrep[rt] = work.tile([P, P], F32, name="sxrep%d" % rt, tag="sxrep", bufs=4)
                 nc.gpsimd.tensor_scalar(out=sxrep[rt][:], in0=ones_f[:], scalar1=sxp[:, rt:rt + 1], scalar2=C / ROWS, op0=ALU.mult, op1=ALU.mult)
-
-        def rsx(rt):
-            if SX[rt] == "P":
-                nc.vector.tensor_reduce(out=sxr[:, rt * P:(rt + 1) * P], in_=tb[("s", rt)][:].rearrange("p (r t) -> p r t", t=4),
-                                        axis=AX.X, op=ALU.add)
 
         def sx_spread():
             rts = [rt for rt in range(4) if SX[rt] != "P"]
@@ -190,30 +197,42 @@ def tile_optimalnet_pa_kernel(tc, x, W1, b1, W2, b2, out_0, out_1, out_2):
                 if SX[rt] == "P":
                     nc.vector.tensor_scalar(out=sxc[:, rt * P:(rt + 1) * P], in0=sxr[:, rt * P:(rt + 1) * P], scalar1=C / ROWS, scalar2=None, op0=ALU.mult)
 
-        def perm(b, es=(0, 1)):
-            for e in es:
-                if (b, e) in PERM:
-                    if b not in pw:
-                        pw[b] = stage.tile([P, 2048], F32, name="pw%d" % b, tag="pw", bufs=NPW)
-                    if b == 0:
-                        for r in range(2):
-                            copy_on(PERM[(b, e)], pw[b][:, r * 1024:(r + 1) * 1024].rearrange("p (u h n i) -> p h u n i", u=2, h=2, i=2)[:, e],
-                                    wt[b][:, r * 2048 + e * 1024:r * 2048 + (e + 1) * 1024].bitcast(F32).rearrange("p (n u i) -> p u n i", u=2, i=2))
-                    else:
-                        pairs(PERM[(b, e)], pw[b][:, e * 1024:(e + 1) * 1024], wt[b][:, e * 2048:(e + 1) * 2048].bitcast(F32))
+        def perm(b, which=(0, 1)):
+            if b not in pw:
+                pw[b] = stage.tile([P, 2048], F32, name="pw%d" % b, tag="pw", bufs=NPW)
+            w32 = wt[b][:].bitcast(F32)
+            if b < 8:
+                for g0, n, eng in RUNS:
+                    if b == 0 and g0 // 2 not in which:
+                        continue
+                    for i in range(2):
+                        lo = i * 1024 + g0 * 256
+                        pairs(eng, pw[b][:, lo:lo + n * 256], w32[:, lo:lo + n * 256])
+                        for g in range(g0, g0 + n):
+                            for u in range(2):
+                                at = lo + u * n * P + (g - g0) * P
+                                ps[(b, g, i, u)] = pw[b][:, at:at + P]
+            else:
+                for e in range(2):
+                    pairs(PERM[(b, e)], pw[b][:, e * 1024:(e + 1) * 1024], w32[:, e * 1024:(e + 1) * 1024])
+                    for g in range(4):
+                        for u in range(2):
+                            ps[(b, g, e, u)] = pw[b][:, e * 1024 + u * 512 + g * P:e * 1024 + u * 512 + (g + 1) * P]
 
         def tw(b, which=(0, 1, 2, 3)):
             w32 = wt[b][:].bitcast(F32)
+
+            def src(g, i, u):
+                at = i * 1024 + g * 256 + u
+                return ps.get((b, g, i, u), w32[:, at:at + 255:2])
+
             for i in which:
                 bank = psT.tile([P, 512], F32, name="tw%d_%d" % (b, i), tag="T")
                 if b < 8:
-                    if L1PAIR:
-                        four_transposes(bank, pw[b], [r * 1024 + u * 512 + i * P for r in range(2) for u in range(2)], 1, identp)
-                    else:
-                        four_transposes(bank, w32, [r * 1024 + i * 256 + u for r in range(2) for u in range(2)], 2, identp)
+                    four_transposes(bank, [src(i, r, u) for r in range(2) for u in range(2)], identp)
                 else:
                     e, gp = i // 2, i % 2
-                    four_transposes(bank, pw[b], [e * 1024 + u * 512 + (2 * gp + gl) * P for gl in range(2) for u in range(2)], 1, ident)
+                    four_transposes(bank, [src(g, e, u) for g in (2 * gp, 2 * gp + 1) for u in range(2)], ident)
                 tb[(b, i)] = bank
 
         def ew(b, i, eng):
@@ -246,6 +265,16 @@ def tile_optimalnet_pa_kernel(tc, x, W1, b1, W2, b2, out_0, out_1, out_2):
                                         rhs=rc[:, g * 512:(g + 1) * 512].bitcast(FP8X4), rhs_scale=rs[:, g * 512:(g + 1) * 512],
                                         start=(g == 0), stop=(g == 3))
 
+        def mm_half(h):
+            for e in range(2):
+                if h == 0:
+                    mb[(0, e)] = psM.tile([P, 512], F32, name="m0_%d" % e, tag="M")
+                for g in range(4):
+                    lo, at = (g * 2 + e) * P, g * 512 + h * 256
+                    nc.tensor.matmul_mx(out=mb[(0, e)][:, h * 256:(h + 1) * 256], lhsT=wc[0][:, lo:lo + P].bitcast(FP8X4),
+                                        lhsT_scale=ws[0][:, lo:lo + P], rhs=xc[:, at:at + 256].bitcast(FP8X4), rhs_scale=xsc[:, at:at + 256],
+                                        start=(g == 0), stop=(g == 3))
+
         def msum(b, e):
             col = (2 * e + b % 2) * P + b // 2 if b < 8 else (b - 8) * 2 + e
             return mp[b // 8][:, col:col + 1]
@@ -255,13 +284,14 @@ def tile_optimalnet_pa_kernel(tc, x, W1, b1, W2, b2, out_0, out_1, out_2):
             vt[(b, e)] = work.tile([P, ROWS], F32, name="v%d_%d" % (b, e), tag="v", bufs=NV)
             nc.scalar.activation(out=vt[(b, e)][:], in_=mb[(b, e)][:], func=ACT.Relu, bias=biasf[:, j:j + 1], scale=1.0,
                                  accum_out=msum(b, e))
+            if b < 8:
+                pending.append((b, e))
 
             if b >= 8:
-                rep[(b, e)] = work.tile([P, P], F32, name="rep%d_%d" % (b, e), tag="rep", bufs=6)
+                rep[(b, e)] = work.tile([P, P], F32, name="rep%d_%d" % (b, e), tag="rep", bufs=RB)
                 eng = nc.gpsimd if b < REPG else nc.vector
                 eng.tensor_scalar(out=rep[(b, e)][:], in0=ones_f[:], scalar1=msum(b, e), scalar2=1.0 / ROWS, op0=ALU.mult, op1=ALU.mult)
 
-        pending = []
         added = [0]
 
         def hh(b, e):
@@ -270,7 +300,6 @@ def tile_optimalnet_pa_kernel(tc, x, W1, b1, W2, b2, out_0, out_1, out_2):
                 hcn[g] = work.tile([P, 2048], BF16, name="hcn%d" % g, tag="hcn")
             nc.vector.scalar_tensor_tensor(out=hcn[g][:, t * ROWS:(t + 1) * ROWS], in0=sxc[:], scalar=msum(b, e), in1=vt[(b, e)][:],
                                            op0=ALU.mult, op1=ALU.add)
-            pending.append((b, e))
 
         def adds(n):
             for i in range(n):
@@ -354,13 +383,14 @@ def tile_optimalnet_pa_kernel(tc, x, W1, b1, W2, b2, out_0, out_1, out_2):
             ex(rt, 0, engines[0])
             ex(rt, 1, engines[1])
 
+        bzp = const.tile([P, 256], F32, name="bzp")
+        pairs("V", bzp[:], bz[:].bitcast(F32))
         xperm(0)
         txe(0, HX[0])
+        sx(0)
         warm_up(WARM1)
         xperm(1)
         bank = psT.tile([P, 512], F32, name="tbias", tag="T")
-        bzp = const.tile([P, 256], F32, name="bzp")
-        pairs("V", bzp[:], bz[:].bitcast(F32))
         for h in range(2):
             nc.tensor.transpose(out=bank[:, h * P:(h + 1) * P], in_=bzp[:, h * P:(h + 1) * P], identity=ident[:])
         nc.tensor.transpose(out=bank[:, 2 * P:3 * P], in_=bz[:].bitcast(F32)[:, 0:P], identity=ident[:])
@@ -368,48 +398,44 @@ def tile_optimalnet_pa_kernel(tc, x, W1, b1, W2, b2, out_0, out_1, out_2):
         nc.vector.tensor_copy(out=bw[:, 8:16], in_=bank[:, 2 * P + 4:2 * P + 12])
         nc.vector.tensor_copy(out=biasf[:], in_=bw[:].bitcast(BF16))
         txe(1, HX[1])
-        warm_up(1, DN)
-        sx(0)
+        warm_up(WA)
+        perm(0, (0,))
         qx(0)
-        xperm(2)
-        txe(2, HX[2])
-        warm_up(1, DN)
+        tw(0, (0, 1))
+        ew(0, 0, HW[0])
+        ew(0, 1, HW[1])
+        warm_up(WB)
+        perm(0, (1,))
         sx(1)
         load(NW - 2)
         qx(1)
-        perm(0, (0,))
-        tw(0, (0, 1))
-        warm_up(1, DN)
-        ew(0, 0, HW[0])
-        ew(0, 1, HW[1])
-        xperm(3)
-        qx(2)
-        txe(3, HX[3])
-        warm_up(1, DN)
-        perm(0, (1,))
-        qw(0, 0)
         tw(0, (2, 3))
-        warm_up(1, DN)
         ew(0, 2, HW[2])
         ew(0, 3, HW[3])
-        warm_up(DW)
-        qx(3)
-        perm(1)
+        warm_up(WC)
+        qw(0, 0)
+        xperm(2)
+        txe(2, HX[2])
+        warm_up(WD)
+        xperm(3)
         qw(0, 1)
+        txe(3, HX[3])
+        warm_up(DW)
+        qx(2)
+        mm_half(0)
+        perm(1)
+        qx(3)
         sx(2)
-        sx(3)
-        load(NW - 1)
-        load(NW)
-        perm(2)
 
-        done_t, done_q, done_p = 0, 0, 2
+        done_t, done_q, done_p = 0, 0, 1
+        done_h = 0
         sh_step = 99
         turned = [8]
         b = 0
 
         def turn_some():
             for i in range(TPS):
-                if b >= sh_step + SHL + (0 if TPOS == 1 else 1) and turned[0] <= min(15, b - 1):
+                if b >= sh_step + SHL + 1 and turned[0] <= min(15, b - 1):
                     to(turned[0])
                     em(turned[0])
                     if turned[0] == 15:
@@ -421,49 +447,48 @@ def tile_optimalnet_pa_kernel(tc, x, W1, b1, W2, b2, out_0, out_1, out_2):
             prev = b - 1
             ahead = min(15, b + AHEAD[min(b, 19)])
             t_list = list(range(done_t + 1, ahead + 1))
+            late = t_list[1:] if b == 8 else []
             if 0 <= prev <= 15:
                 act(prev, 1)
-            if TPOS == 2:
-                turn_some()
-            if b == 1:
-                for rt in range(4):
-                    rsx(rt)
+            turn_some()
+            if b == SPREAD:
                 sx_spread()
-                hh(0, 0)
-            if 0 <= prev <= 7:
-                hh(prev, 1)
-                if prev % 2 == 1:
-                    rg(prev // 2)
+            fresh = []
+            for i in range(HHN[b] if b < 9 else 0):
+                n = done_h
+                hh(n // 2, n % 2)
+                done_h = n + 1
+                if n % 4 == 3:
+                    rg(n // 4)
+                    fresh.append(n // 4)
             if b == 8:
                 qh(3)
             for t in range(done_q + 1, done_t + 1):
                 qw(t)
                 done_q = t
-            if len(t_list) > 0:
-                t = t_list[0]
-                tw(t)
-                load(t + NW)
-                done_t = t
-                for i in range(4):
-                    ew(t, i, EWE[t][i])
+            for t in t_list:
+                if t not in late:
+                    tw(t)
+                    if b > 0:
+                        load(t + NW)
+                    done_t = t
+                    for i in range(4):
+                        ew(t, i, EWE[t][i])
             need_p = min(15, max(ahead, b + 1 + AHEAD[min(b + 1, 19)]))
-            for t in range(done_p + 1, need_p + 1):
-                perm(t)
-                done_p = t
-            if prev % 2 == 1 and 0 < prev < 7:
-                qh(prev // 2)
-            if TPOS == 0:
-                turn_some()
+            if done_p < need_p:
+                done_p = done_p + 1
+                perm(done_p)
+            if b < 8:
+                for g in fresh:
+                    qh(g)
             if b == 9:
                 mout1()
             if b == 0:
-                mm(0, (0,))
+                mm_half(1)
                 act(0, 0)
-                mm(0, (1,))
-                pass
             elif b == 8:
                 mm(8, (0, 1), (0, 1, 2))
-                for t in t_list[1:]:
+                for t in late:
                     tw(t)
                     load(t + NW)
                     done_t = t
@@ -476,15 +501,18 @@ def tile_optimalnet_pa_kernel(tc, x, W1, b1, W2, b2, out_0, out_1, out_2):
                 act(b, 0)
             if b == sh_step + SHL:
                 sh_rest()
-            if TPOS == 1:
-                turn_some()
             if b + 1 <= 15 and done_q < b + 1:
                 qw(b + 1)
                 done_q = b + 1
-            if 0 < b <= 7:
-                hh(b, 0)
+            if b == 0:
+                sx(3)
+                for t in range(NW - 1, done_t + NW + 1):
+                    load(t)
+            while done_p < need_p:
+                done_p = done_p + 1
+                perm(done_p)
             if sh_step == 99:
-                adds(ADD[b])
+                adds(ADD[b] if b < len(ADD) else 2)
                 if added[0] == 14:
                     sh_vector()
                     sh_step = b

@@ -25,22 +25,23 @@ WARM1 = 2
 RUNS = []
 XRUNS = []
 PAIRED = [g for g0, n, eng in RUNS for g in range(g0, g0 + n)]
-PERM = {(b, e): "S" if (b, e) in ((9, 1), (10, 0)) else "V" for b in range(8, 16) for e in range(2)}
+PERM = {(b, e): "V" for b in range(8, 16) for e in range(2)}
 XP = "VVVV"
-ADD = [0, 1, 2, 2, 1, 1, 1, 2, 2, 2]
+ADD = [0, 1, 2, 2, 2, 1, 0, 0, 0, 3, 3]
 AHEAD = [1] * 8 + [2] * 12
 SX = "VVVV"
 HX = ["SS", "SS", "SS", "SS"]
 HW = "SSSS"
 SHL = 1
-TPS = 1
+SPLIT = [0] * 16
+TMID = 1
+CL = 1
+TPS = 2
 EWE = ["SSSS"] * 16
-REPG = 14
 WA, WB, WC, WD = 2, 1, 1, 1
-SPREAD = 3
-HHN = [0, 0, 0, 4, 3, 3, 2, 2, 2]
+SPREAD = 2
+HHN = [0, 0, 4, 2, 2, 2, 2, 2, 2]
 DW = 0
-RB = 10
 
 
 def tile_optimalnet_pa_kernel(tc, x, W1, b1, W2, b2, out_0, out_1, out_2):
@@ -88,8 +89,9 @@ def tile_optimalnet_pa_kernel(tc, x, W1, b1, W2, b2, out_0, out_1, out_2):
         nc.gpsimd.tensor_copy(out=identp[:].rearrange("p (u j) -> p u j", u=2), in_=ident[:].rearrange("p (j u) -> p u j", u=2))
         ones_f = const.tile([P, P], F32, name="ones_f")
         nc.vector.memset(ones_f[:], 1.0)
-        mp = [const.tile([P, 512], F32, name="mp0"), const.tile([P, 16], F32, name="mp1")]
+        mp = [const.tile([P, 512], F32, name="mp0"), const.tile([P, 256], F32, name="mp1")]
         nc.vector.memset(mp[0][:], 0.0)
+        nc.gpsimd.memset(mp[1][:], 0.0)
         tabl = const.tile([P, 1], F32, name="tabl")
         nc.scalar.activation(out=tabl[:], in_=ones_f[:, 0:1], func=ACT.Relu)
         warm = psM.tile([P, 512], F32, name="warm", tag="M")
@@ -112,14 +114,13 @@ def tile_optimalnet_pa_kernel(tc, x, W1, b1, W2, b2, out_0, out_1, out_2):
         sxc = const.tile([P, ROWS], F32, name="sxc")
         acc = [const.tile([P, ROWS], F32, name="acc0"), const.tile([P, ROWS], F32, name="acc1")]
         accf = const.tile([P, ROWS], F32, name="accf")
-        shc = const.tile([P, 4], F32, name="shc")
+        shb = const.tile([P, ROWS], F32, name="shb")
         s1 = const.tile([P, 1], F32, name="s1")
-        m2b = const.tile([P, 2048], F32, name="m2b")
 
         w1src = W1.rearrange("(g p i e) k -> g e p i k", p=P, i=2, e=2)
         w2src = W2.rearrange("(c p e) k -> c p (e k)", p=P, e=2)
         pending = []
-        pw, ps, wt, tb, gw, wc, ws, mb, vt, ob, hcn, gh, rep = {}, {}, {}, {}, {}, {}, {}, {}, {}, {}, {}, {}, {}
+        pw, ps, wt, tb, gw, wc, ws, mb, vt, ob, hcn, gh = {}, {}, {}, {}, {}, {}, {}, {}, {}, {}, {}, {}
 
         def load(b):
             if b <= 15:
@@ -166,6 +167,11 @@ def tile_optimalnet_pa_kernel(tc, x, W1, b1, W2, b2, out_0, out_1, out_2):
             for g in range(4):
                 lo = g * 512 + rt * P
                 nc.vector.quantize_mx(out=xc[:, lo:lo + P].bitcast(FP8X4), scales=xsc[:, lo:lo + P], in_=gx[:, 4 * lo:4 * (lo + P)])
+
+        def qxh(h):
+            for g in range(4):
+                lo = g * 512 + h * 256
+                nc.vector.quantize_mx(out=xc[:, lo:lo + 256].bitcast(FP8X4), scales=xsc[:, lo:lo + 256], in_=gx[:, 4 * lo:4 * (lo + 256)])
 
         def sx(rt):
             if SX[rt] == "P":
@@ -276,7 +282,7 @@ def tile_optimalnet_pa_kernel(tc, x, W1, b1, W2, b2, out_0, out_1, out_2):
                                         start=(g == 0), stop=(g == 3))
 
         def msum(b, e):
-            col = (2 * e + b % 2) * P + b // 2 if b < 8 else (b - 8) * 2 + e
+            col = (2 * e + b % 2) * P + b // 2 if b < 8 else e * P + b - 8
             return mp[b // 8][:, col:col + 1]
 
         def act(b, e):
@@ -287,10 +293,6 @@ def tile_optimalnet_pa_kernel(tc, x, W1, b1, W2, b2, out_0, out_1, out_2):
             if b < 8:
                 pending.append((b, e))
 
-            if b >= 8:
-                rep[(b, e)] = work.tile([P, P], F32, name="rep%d_%d" % (b, e), tag="rep", bufs=RB)
-                eng = nc.gpsimd if b < REPG else nc.vector
-                eng.tensor_scalar(out=rep[(b, e)][:], in0=ones_f[:], scalar1=msum(b, e), scalar2=1.0 / ROWS, op0=ALU.mult, op1=ALU.mult)
 
         added = [0]
 
@@ -324,15 +326,14 @@ def tile_optimalnet_pa_kernel(tc, x, W1, b1, W2, b2, out_0, out_1, out_2):
 
         def sh_rest():
             bank = psT.tile([P, 512], F32, name="shb", tag="T")
-            for rb in range(4):
-                nc.tensor.matmul(out=bank[:, rb * 32:(rb + 1) * 32], lhsT=accf[:, rb * P:(rb + 1) * P], rhs=ones_f[:, 0:32], start=True, stop=True)
-            nc.scalar.mul(out=shc[:], in_=bank[:, 0:P].rearrange("p (b n) -> p b n", n=32)[:, :, 0], mul=C)
+            nc.tensor.matmul(out=bank[:], lhsT=ones_f[:], rhs=accf[:], start=True, stop=True)
+            nc.scalar.mul(out=shb[:], in_=bank[:], mul=C / ROWS)
+
+        def corr(b):
+            for e in range(2):
+                nc.vector.scalar_tensor_tensor(out=vt[(b, e)][:], in0=shb[:], scalar=msum(b, e), in1=vt[(b, e)][:], op0=ALU.mult, op1=ALU.add)
 
         def to(b):
-            bank = psT.tile([P, 512], F32, name="tr%d" % b, tag="T")
-            for e in range(2):
-                nc.tensor.transpose(out=bank[:, e * P:(e + 1) * P], in_=rep[(b, e)][:], identity=ident[:])
-            tb[("r", b)] = bank
             for k in range(2):
                 bank = psT.tile([P, 512], F32, name="to%d_%d" % (b, k), tag="T")
                 for l in range(2):
@@ -342,27 +343,27 @@ def tile_optimalnet_pa_kernel(tc, x, W1, b1, W2, b2, out_0, out_1, out_2):
                                             identity=ident[:])
                 tb[("o", b, k)] = bank
 
-        def em(b):
-            c = b - 8
-            nc.scalar.copy(out=m2b[:, c * 256:(c + 1) * 256].rearrange("r (p e) -> r p e", e=2),
-                           in_=tb[("r", b)][:, 0:256].rearrange("r (e p) -> r p e", e=2))
-
-        def eo(b):
+        def eo(b, engines="SS"):
             c = b - 8
             ob[b] = work.tile([P, 1024], F32, name="o%d" % b, tag="o", bufs=3)
-            for rb in range(4):
-                k, l = rb // 2, rb % 2
-                nc.vector.scalar_tensor_tensor(out=ob[b][:, rb * 256:(rb + 1) * 256].rearrange("r (p e) -> r p e", e=2),
-                                               in0=m2b[:, c * 256:(c + 1) * 256].rearrange("r (p e) -> r p e", e=2),
-                                               scalar=shc[:, rb:rb + 1],
-                                               in1=tb[("o", b, k)][:, l * 256:(l + 1) * 256].rearrange("r (e p) -> r p e", e=2),
-                                               op0=ALU.mult, op1=ALU.add)
-                if b == 15 and rb % 2 == 1:
-                    nc.sync.dma_start(out=out_0.rearrange("(k r) o -> r k o", r=P)[:, rb - 1:rb + 1, c * 256:(c + 1) * 256],
-                                      in_=ob[b][:].rearrange("r (k o) -> r k o", k=4)[:, rb - 1:rb + 1, :])
+            for k in range(2):
+                copy_on(engines[k], ob[b][:, k * 512:(k + 1) * 512].rearrange("r (l p e) -> r l p e", l=2, e=2),
+                        tb[("o", b, k)][:].rearrange("r (l e p) -> r l p e", l=2, e=2))
+                if b == 15:
+                    nc.sync.dma_start(out=out_0.rearrange("(k r) o -> r k o", r=P)[:, 2 * k:2 * k + 2, c * 256:(c + 1) * 256],
+                                      in_=ob[b][:, k * 512:(k + 1) * 512].rearrange("r (l o) -> r l o", l=2))
             if b < 15:
                 nc.sync.dma_start(out=out_0.rearrange("(k r) o -> r k o", r=P)[:, :, c * 256:(c + 1) * 256],
                                   in_=ob[b][:].rearrange("r (k o) -> r k o", k=4))
+
+        def mout2():
+            bank = psT.tile([P, 512], F32, name="mo2", tag="T")
+            for e in range(2):
+                nc.tensor.transpose(out=bank[:, e * P:(e + 1) * P], in_=mp[1][:, e * P:(e + 1) * P], identity=ident[:])
+            ms2 = work.tile([P, 256], F32, name="ms2", tag="ms2", bufs=1)
+            nc.scalar.activation(out=ms2[:].rearrange("c (p e) -> c p e", e=2), in_=bank[:, 0:256].rearrange("c (e p) -> c p e", e=2),
+                                 func=ACT.Copy, scale=1.0 / ROWS)
+            nc.sync.dma_start(out=out_2.rearrange("(c n) -> c n", n=256), in_=ms2[0:8, :])
 
         def mout1():
             bank = psT.tile([P, 512], F32, name="mo", tag="T")
@@ -399,16 +400,13 @@ def tile_optimalnet_pa_kernel(tc, x, W1, b1, W2, b2, out_0, out_1, out_2):
         nc.vector.tensor_copy(out=biasf[:], in_=bw[:].bitcast(BF16))
         txe(1, HX[1])
         warm_up(WA)
-        perm(0, (0,))
-        qx(0)
         tw(0, (0, 1))
         ew(0, 0, HW[0])
         ew(0, 1, HW[1])
         warm_up(WB)
-        perm(0, (1,))
+        qxh(0)
         sx(1)
         load(NW - 2)
-        qx(1)
         tw(0, (2, 3))
         ew(0, 2, HW[2])
         ew(0, 3, HW[3])
@@ -421,26 +419,34 @@ def tile_optimalnet_pa_kernel(tc, x, W1, b1, W2, b2, out_0, out_1, out_2):
         qw(0, 1)
         txe(3, HX[3])
         warm_up(DW)
-        qx(2)
         mm_half(0)
-        perm(1)
-        qx(3)
+        qxh(1)
         sx(2)
 
         done_t, done_q, done_p = 0, 0, 1
         done_h = 0
         sh_step = 99
+        corrected = [8]
         turned = [8]
         b = 0
 
         def turn_some():
+            ready = corrected[0]
             for i in range(TPS):
-                if b >= sh_step + SHL + 1 and turned[0] <= min(15, b - 1):
+                if turned[0] < ready:
                     to(turned[0])
-                    em(turned[0])
-                    if turned[0] == 15:
-                        nc.sync.dma_start(out=out_2.rearrange("(a n) -> a n", a=1), in_=m2b[0:1, :])
                     eo(turned[0])
+                    turned[0] = turned[0] + 1
+            for i in range(TPS):
+                if b >= sh_step + SHL + CL and corrected[0] <= min(15, b - 1):
+                    corr(corrected[0])
+                    corrected[0] = corrected[0] + 1
+            if b > 15:
+                while turned[0] < corrected[0]:
+                    to(turned[0])
+                    if turned[0] == 15:
+                        mout2()
+                    eo(turned[0], "SV")
                     turned[0] = turned[0] + 1
 
         while turned[0] <= 15:
@@ -450,7 +456,8 @@ def tile_optimalnet_pa_kernel(tc, x, W1, b1, W2, b2, out_0, out_1, out_2):
             late = t_list[1:] if b == 8 else []
             if 0 <= prev <= 15:
                 act(prev, 1)
-            turn_some()
+            if not TMID:
+                turn_some()
             if b == SPREAD:
                 sx_spread()
             fresh = []
@@ -466,8 +473,14 @@ def tile_optimalnet_pa_kernel(tc, x, W1, b1, W2, b2, out_0, out_1, out_2):
             for t in range(done_q + 1, done_t + 1):
                 qw(t)
                 done_q = t
+            split = SPLIT[b] if 1 <= b <= 15 and b != 8 and len(t_list) == 1 else 0
+            if split:
+                t = t_list[0]
+                tw(t, (0, 1))
+                for i in range(2):
+                    ew(t, i, EWE[t][i])
             for t in t_list:
-                if t not in late:
+                if t not in late and not split:
                     tw(t)
                     if b > 0:
                         load(t + NW)
@@ -497,8 +510,20 @@ def tile_optimalnet_pa_kernel(tc, x, W1, b1, W2, b2, out_0, out_1, out_2):
                 mm(8, (0, 1), (3,))
                 act(8, 0)
             elif b <= 15:
-                mm(b)
+                mm(b, (0,))
                 act(b, 0)
+                if split:
+                    t = t_list[0]
+                    tw(t, (2, 3))
+                    load(t + NW)
+                    done_t = t
+                    for i in range(2, 4):
+                        ew(t, i, EWE[t][i])
+                if TMID:
+                    turn_some()
+                mm(b, (1,))
+            elif TMID:
+                turn_some()
             if b == sh_step + SHL:
                 sh_rest()
             if b + 1 <= 15 and done_q < b + 1:

@@ -19,28 +19,27 @@ FLOPS = 2 * 2 * 512 * 2048 * 2048
 
 NW = 6
 NV = 16
-NPW = 2
+NPW = 3
 WARM0 = 4
 WARM1 = 2
-RUNS = []
-XRUNS = []
-PAIRED = [g for g0, n, eng in RUNS for g in range(g0, g0 + n)]
-PERM = {(b, e): "V" for b in range(8, 16) for e in range(2)}
-XP = "VVVV"
-ADD = [0, 1, 2, 2, 2, 1, 0, 0, 0, 3, 3]
+PERM = {}
+SQ = {3: [(8, 0, 0)], 4: [(8, 0, 1)], 5: [(8, 1, 0)], 6: [(8, 1, 1)], 7: [(9, 0, 0), (9, 0, 1)]}
+QUARTERED = [(b, e) for qs in SQ.values() for b, e, q in qs]
+ADD = [0, 1, 2, 2, 2, 1, 1, 0, 1, 2, 2]
 AHEAD = [1] * 8 + [2] * 12
-SX = "VVVV"
+SX = "VPVP"
 HX = ["SS", "SS", "SS", "SS"]
 HW = "SSSS"
 SHL = 1
 SPLIT = [0] * 16
 TMID = 1
+ECORR = 1
 CL = 1
 TPS = 2
 EWE = ["SSSS"] * 16
 WA, WB, WC, WD = 2, 1, 1, 1
-SPREAD = 2
-HHN = [0, 0, 4, 2, 2, 2, 2, 2, 2]
+SPREAD = 1
+HHN = [0, 2, 2, 2, 2, 2, 2, 2, 2]
 DW = 0
 
 
@@ -120,7 +119,7 @@ def tile_optimalnet_pa_kernel(tc, x, W1, b1, W2, b2, out_0, out_1, out_2):
         w1src = W1.rearrange("(g p i e) k -> g e p i k", p=P, i=2, e=2)
         w2src = W2.rearrange("(c p e) k -> c p (e k)", p=P, e=2)
         pending = []
-        pw, ps, wt, tb, gw, wc, ws, mb, vt, ob, hcn, gh = {}, {}, {}, {}, {}, {}, {}, {}, {}, {}, {}, {}
+        pw, wt, tb, gw, wc, ws, mb, vt, ob, hcn, gh = {}, {}, {}, {}, {}, {}, {}, {}, {}, {}, {}
 
         def load(b):
             if b <= 15:
@@ -138,24 +137,13 @@ def tile_optimalnet_pa_kernel(tc, x, W1, b1, W2, b2, out_0, out_1, out_2):
         def pairs(eng, out, in_):
             copy_on(eng, out.rearrange("p (u n i) -> p u n i", u=2, i=2), in_.rearrange("p (n u i) -> p u n i", u=2, i=2))
 
-        pxt = {}
         sxrep = {}
-
-        def xperm(rt):
-            pxt[rt] = {}
-            for g0, n, eng in XRUNS:
-                px = stage.tile([P, n * 256], F32, name="px%d_%d" % (rt, g0), tag="px%d" % g0, bufs=2)
-                lo = (rt % 2) * 1024 + g0 * 256
-                pairs(eng, px[:], xt[rt // 2][:].bitcast(F32)[:, lo:lo + n * 256])
-                for g in range(g0, g0 + n):
-                    for u in range(2):
-                        pxt[rt][(g, u)] = px[:, u * n * P + (g - g0) * P:u * n * P + (g - g0 + 1) * P]
 
         def tx(rt):
             x32 = xt[rt // 2][:].bitcast(F32)
             for gp in range(2):
                 bank = psT.tile([P, 512], F32, name="tx%d_%d" % (rt, gp), tag="T")
-                four_transposes(bank, [pxt[rt].get((g, u), x32[:, (rt % 2) * 1024 + g * 256 + u:(rt % 2) * 1024 + g * 256 + u + 255:2])
+                four_transposes(bank, [x32[:, (rt % 2) * 1024 + g * 256 + u:(rt % 2) * 1024 + g * 256 + u + 255:2]
                                        for g in (2 * gp, 2 * gp + 1) for u in range(2)], ident)
                 tb[("x", rt, gp)] = bank
 
@@ -182,7 +170,7 @@ def tile_optimalnet_pa_kernel(tc, x, W1, b1, W2, b2, out_0, out_1, out_2):
                 nc.vector.tensor_reduce(out=sxr[:, rt * P:(rt + 1) * P], in_=bank[:].rearrange("p (r t) -> p r t", t=4),
                                         axis=AX.X, op=ALU.add)
             else:
-                junk = stage.tile([P, 2048], BF16, name="jk%d" % rt, tag="jk" + SX[rt], bufs=1)
+                junk = stage.tile([P, 2048], BF16, name="jk%d" % rt, tag="pw", bufs=NPW)
                 src = xt[rt // 2][:, (rt % 2) * 2048:(rt % 2) * 2048 + 2048]
                 if SX[rt] == "V":
                     nc.vector.tensor_scalar(out=junk[:], in0=src, scalar1=1.0, scalar2=0.0, op0=ALU.mult, op1=ALU.add, accum_out=sxp[:, rt:rt + 1])
@@ -194,43 +182,39 @@ def tile_optimalnet_pa_kernel(tc, x, W1, b1, W2, b2, out_0, out_1, out_2):
         def sx_spread():
             rts = [rt for rt in range(4) if SX[rt] != "P"]
             if len(rts) > 0:
-                lo, hi = rts[0] * P, (rts[-1] + 1) * P
                 bank = psT.tile([P, 512], F32, name="sxb", tag="T")
                 for rt in rts:
                     nc.tensor.transpose(out=bank[:, rt * P:(rt + 1) * P], in_=sxrep[rt][:], identity=ident[:])
-                nc.scalar.copy(out=sxc[:, lo:hi], in_=bank[:, lo:hi])
+                for rt in rts:
+                    nc.scalar.copy(out=sxc[:, rt * P:(rt + 1) * P], in_=bank[:, rt * P:(rt + 1) * P])
             for rt in range(4):
                 if SX[rt] == "P":
                     nc.vector.tensor_scalar(out=sxc[:, rt * P:(rt + 1) * P], in0=sxr[:, rt * P:(rt + 1) * P], scalar1=C / ROWS, scalar2=None, op0=ALU.mult)
 
-        def perm(b, which=(0, 1)):
+        def pw_tile(b):
             if b not in pw:
                 pw[b] = stage.tile([P, 2048], F32, name="pw%d" % b, tag="pw", bufs=NPW)
-            w32 = wt[b][:].bitcast(F32)
-            if b < 8:
-                for g0, n, eng in RUNS:
-                    if b == 0 and g0 // 2 not in which:
-                        continue
-                    for i in range(2):
-                        lo = i * 1024 + g0 * 256
-                        pairs(eng, pw[b][:, lo:lo + n * 256], w32[:, lo:lo + n * 256])
-                        for g in range(g0, g0 + n):
-                            for u in range(2):
-                                at = lo + u * n * P + (g - g0) * P
-                                ps[(b, g, i, u)] = pw[b][:, at:at + P]
-            else:
+            return pw[b]
+
+        def perm(b):
+            if b >= 8:
                 for e in range(2):
-                    pairs(PERM[(b, e)], pw[b][:, e * 1024:(e + 1) * 1024], w32[:, e * 1024:(e + 1) * 1024])
-                    for g in range(4):
-                        for u in range(2):
-                            ps[(b, g, e, u)] = pw[b][:, e * 1024 + u * 512 + g * P:e * 1024 + u * 512 + (g + 1) * P]
+                    if (b, e) not in QUARTERED:
+                        pairs(PERM.get((b, e), "V"), pw_tile(b)[:, e * 1024:(e + 1) * 1024], wt[b][:, e * 2048:(e + 1) * 2048].bitcast(F32))
+
+        def perm_quarter(b, e, q):
+            copy_on("S", pw_tile(b)[:, e * 1024:(e + 1) * 1024].rearrange("p (u q n i) -> p q u n i", u=2, q=2, i=2)[:, q],
+                    wt[b][:, e * 2048 + q * 1024:e * 2048 + (q + 1) * 1024].bitcast(F32).rearrange("p (n u i) -> p u n i", u=2, i=2))
 
         def tw(b, which=(0, 1, 2, 3)):
             w32 = wt[b][:].bitcast(F32)
 
             def src(g, i, u):
-                at = i * 1024 + g * 256 + u
-                return ps.get((b, g, i, u), w32[:, at:at + 255:2])
+                if b < 8:
+                    at = i * 1024 + g * 256 + u
+                    return w32[:, at:at + 255:2]
+                at = i * 1024 + u * 512 + g * P
+                return pw[b][:, at:at + P]
 
             for i in which:
                 bank = psT.tile([P, 512], F32, name="tw%d_%d" % (b, i), tag="T")
@@ -329,30 +313,28 @@ def tile_optimalnet_pa_kernel(tc, x, W1, b1, W2, b2, out_0, out_1, out_2):
             nc.tensor.matmul(out=bank[:], lhsT=ones_f[:], rhs=accf[:], start=True, stop=True)
             nc.scalar.mul(out=shb[:], in_=bank[:], mul=C / ROWS)
 
-        def corr(b):
-            for e in range(2):
+        def corr(b, es=(0, 1)):
+            for e in es:
                 nc.vector.scalar_tensor_tensor(out=vt[(b, e)][:], in0=shb[:], scalar=msum(b, e), in1=vt[(b, e)][:], op0=ALU.mult, op1=ALU.add)
 
         def to(b):
             for k in range(2):
-                bank = psT.tile([P, 512], F32, name="to%d_%d" % (b, k), tag="T")
-                for l in range(2):
-                    for e in range(2):
-                        rb = 2 * k + l
-                        nc.tensor.transpose(out=bank[:, (l * 2 + e) * P:(l * 2 + e + 1) * P], in_=vt[(b, e)][:, rb * P:(rb + 1) * P],
-                                            identity=ident[:])
-                tb[("o", b, k)] = bank
+                tb[("o", b, k)] = psT.tile([P, 512], F32, name="to%d_%d" % (b, k), tag="T")
+            for e in range(2):
+                for rb in range(4):
+                    at = ((rb % 2) * 2 + e) * P
+                    nc.tensor.transpose(out=tb[("o", b, rb // 2)][:, at:at + P], in_=vt[(b, e)][:, rb * P:(rb + 1) * P], identity=ident[:])
 
         def eo(b, engines="SS"):
             c = b - 8
-            ob[b] = work.tile([P, 1024], F32, name="o%d" % b, tag="o", bufs=3)
+            ob[b] = work.tile([P, 1024], F32, name="o%d" % b, tag="o", bufs=4)
             for k in range(2):
                 copy_on(engines[k], ob[b][:, k * 512:(k + 1) * 512].rearrange("r (l p e) -> r l p e", l=2, e=2),
                         tb[("o", b, k)][:].rearrange("r (l e p) -> r l p e", l=2, e=2))
-                if b == 15:
+                if b >= 13:
                     nc.sync.dma_start(out=out_0.rearrange("(k r) o -> r k o", r=P)[:, 2 * k:2 * k + 2, c * 256:(c + 1) * 256],
                                       in_=ob[b][:, k * 512:(k + 1) * 512].rearrange("r (l o) -> r l o", l=2))
-            if b < 15:
+            if b < 13:
                 nc.sync.dma_start(out=out_0.rearrange("(k r) o -> r k o", r=P)[:, :, c * 256:(c + 1) * 256],
                                   in_=ob[b][:].rearrange("r (k o) -> r k o", k=4))
 
@@ -386,11 +368,9 @@ def tile_optimalnet_pa_kernel(tc, x, W1, b1, W2, b2, out_0, out_1, out_2):
 
         bzp = const.tile([P, 256], F32, name="bzp")
         pairs("V", bzp[:], bz[:].bitcast(F32))
-        xperm(0)
         txe(0, HX[0])
         sx(0)
         warm_up(WARM1)
-        xperm(1)
         bank = psT.tile([P, 512], F32, name="tbias", tag="T")
         for h in range(2):
             nc.tensor.transpose(out=bank[:, h * P:(h + 1) * P], in_=bzp[:, h * P:(h + 1) * P], identity=ident[:])
@@ -412,12 +392,12 @@ def tile_optimalnet_pa_kernel(tc, x, W1, b1, W2, b2, out_0, out_1, out_2):
         ew(0, 3, HW[3])
         warm_up(WC)
         qw(0, 0)
-        xperm(2)
         txe(2, HX[2])
         warm_up(WD)
-        xperm(3)
         qw(0, 1)
         txe(3, HX[3])
+        if SX[3] == "S":
+            sx(3)
         warm_up(DW)
         mm_half(0)
         qxh(1)
@@ -432,29 +412,30 @@ def tile_optimalnet_pa_kernel(tc, x, W1, b1, W2, b2, out_0, out_1, out_2):
 
         def turn_some():
             ready = corrected[0]
+            later = []
             for i in range(TPS):
                 if turned[0] < ready:
                     to(turned[0])
-                    eo(turned[0])
+                    if b == 15 and i == TPS - 1:
+                        later.append(turned[0])
+                    else:
+                        eo(turned[0])
                     turned[0] = turned[0] + 1
             for i in range(TPS):
-                if b >= sh_step + SHL + CL and corrected[0] <= min(15, b - 1):
+                if b >= sh_step + SHL + CL and corrected[0] <= b - 1:
                     corr(corrected[0])
                     corrected[0] = corrected[0] + 1
-            if b > 15:
-                while turned[0] < corrected[0]:
-                    to(turned[0])
-                    if turned[0] == 15:
-                        mout2()
-                    eo(turned[0], "SV")
-                    turned[0] = turned[0] + 1
+            if b == 15:
+                corr(15, (0,))
+            for t in later:
+                eo(t, "VV")
 
-        while turned[0] <= 15:
+        while b <= 15:
             prev = b - 1
             ahead = min(15, b + AHEAD[min(b, 19)])
             t_list = list(range(done_t + 1, ahead + 1))
             late = t_list[1:] if b == 8 else []
-            if 0 <= prev <= 15:
+            if 0 <= prev:
                 act(prev, 1)
             if not TMID:
                 turn_some()
@@ -512,6 +493,8 @@ def tile_optimalnet_pa_kernel(tc, x, W1, b1, W2, b2, out_0, out_1, out_2):
             elif b <= 15:
                 mm(b, (0,))
                 act(b, 0)
+                for qb, qe, qq in SQ.get(b, []):
+                    perm_quarter(qb, qe, qq)
                 if split:
                     t = t_list[0]
                     tw(t, (2, 3))
@@ -522,15 +505,14 @@ def tile_optimalnet_pa_kernel(tc, x, W1, b1, W2, b2, out_0, out_1, out_2):
                 if TMID:
                     turn_some()
                 mm(b, (1,))
-            elif TMID:
-                turn_some()
             if b == sh_step + SHL:
                 sh_rest()
             if b + 1 <= 15 and done_q < b + 1:
                 qw(b + 1)
                 done_q = b + 1
             if b == 0:
-                sx(3)
+                if SX[3] != "S":
+                    sx(3)
                 for t in range(NW - 1, done_t + NW + 1):
                     load(t)
             while done_p < need_p:
@@ -542,3 +524,16 @@ def tile_optimalnet_pa_kernel(tc, x, W1, b1, W2, b2, out_0, out_1, out_2):
                     sh_vector()
                     sh_step = b
             b = b + 1
+
+        act(15, 1)
+        last = corrected[0]
+        for t in range(last, 15):
+            corr(t)
+        if ECORR:
+            corr(15, (1,))
+        else:
+            corr(15)
+        for t in range(turned[0], 16):
+            to(t)
+            eo(t, "SV")
+        mout2()

@@ -23,7 +23,7 @@ NPW = 3
 WARM0 = 4
 WARM1 = 2
 PERM = {}
-SQ = {3: [(8, 0, 0)], 4: [(8, 0, 1)], 5: [(8, 1, 0)], 6: [(8, 1, 1)], 7: [(9, 0, 0), (9, 0, 1)]}
+SQ = {3: [(8, 0, 0)], 4: [(8, 0, 1)], 5: [(8, 1, 0)], 6: [(8, 1, 1)]}
 QUARTERED = [(b, e) for qs in SQ.values() for b, e, q in qs]
 ADD = [0, 1, 2, 2, 2, 1, 1, 0, 1, 2, 2]
 AHEAD = [1] * 8 + [2] * 12
@@ -31,6 +31,7 @@ SX = "VPVP"
 HX = ["SS", "SS", "SS", "SS"]
 HW = "SSSS"
 SHL = 1
+MO = 9
 SPLIT = [0] * 16
 TMID = 1
 ECORR = 1
@@ -475,7 +476,7 @@ def tile_optimalnet_pa_kernel(tc, x, W1, b1, W2, b2, out_0, out_1, out_2):
             if b < 8:
                 for g in fresh:
                     qh(g)
-            if b == 9:
+            if b == MO:
                 mout1()
             if b == 0:
                 mm_half(1)
@@ -536,4 +537,6 @@ def tile_optimalnet_pa_kernel(tc, x, W1, b1, W2, b2, out_0, out_1, out_2):
         for t in range(turned[0], 16):
             to(t)
             eo(t, "SV")
+        if MO > 15:
+            mout1()
         mout2()

@@ -27,7 +27,7 @@ SQ = {3: [(8, 0, 0)], 4: [(8, 0, 1)], 5: [(8, 1, 0)], 6: [(8, 1, 1)]}
 QUARTERED = [(b, e) for qs in SQ.values() for b, e, q in qs]
 ADD = [0, 1, 2, 2, 2, 1, 1, 0, 1, 2, 2]
 AHEAD = [1] * 8 + [2] * 12
-SX = "VPVP"
+SX = "VVVP"
 HX = ["SS", "SS", "SS", "SS"]
 HW = "SSSS"
 SHL = 1

@@ -14,529 +14,406 @@ AX = mybir.AxisListType
 
 P = 128
 ROWS = 512
+GROUPS = 4
+BATCHES = 16
+FIRST2 = 8
+LAST = BATCHES - 1
 C = 0.01 * 0.001 / 1
-FLOPS = 2 * 2 * 512 * 2048 * 2048
 
-NW = 6
-NV = 16
-NPW = 3
-WARM0 = 4
-WARM1 = 2
-PERM = {}
-SQ = {3: [(8, 0, 0)], 4: [(8, 0, 1)], 5: [(8, 1, 0)], 6: [(8, 1, 1)]}
-QUARTERED = [(b, e) for qs in SQ.values() for b, e, q in qs]
-ADD = [0, 1, 2, 2, 2, 1, 1, 0, 1, 2, 2]
-AHEAD = [1] * 8 + [2] * 12
-SX = "VVVP"
-HX = ["SS", "SS", "SS", "SS"]
-HW = "SSSS"
-SHL = 1
-MO = 9
-SPLIT = [0] * 16
-TMID = 1
-ECORR = 1
-CL = 1
-TPS = 2
-EWE = ["SSSS"] * 16
-WA, WB, WC, WD = 2, 1, 1, 1
-SPREAD = 1
-HHN = [0, 2, 2, 2, 2, 2, 2, 2, 2]
-DW = 0
+IN_BUFS = 6
+SORT_BUFS = 3
+V_BUFS = 16
+OUT_BUFS = 4
+T_BANKS, M_BANKS = 6, 2
+
+ADDS_END = 10
+CORRECT_FROM = 12
 
 
 def tile_optimalnet_pa_kernel(tc, x, W1, b1, W2, b2, out_0, out_1, out_2):
     nc = tc.nc
     with ExitStack() as ctx:
         const = ctx.enter_context(tc.tile_pool(name="const", bufs=1))
-        win = ctx.enter_context(tc.tile_pool(name="win", bufs=NW))
+        arrive = ctx.enter_context(tc.tile_pool(name="arrive", bufs=IN_BUFS))
         stage = ctx.enter_context(tc.tile_pool(name="stage", bufs=3))
         work = ctx.enter_context(tc.tile_pool(name="work", bufs=2))
-        psT = ctx.enter_context(tc.psum_pool(name="psT", bufs=6))
-        psM = ctx.enter_context(tc.psum_pool(name="psM", bufs=2))
+        psT = ctx.enter_context(tc.psum_pool(name="psT", bufs=T_BANKS))
+        psM = ctx.enter_context(tc.psum_pool(name="psM", bufs=M_BANKS))
         ctx.enter_context(tc.manual_schedule())
 
-        def copy_on(eng, out, in_):
-            if eng == "V":
+        def copy_on(engine, out, in_):
+            if engine == "V":
                 nc.vector.tensor_copy(out=out, in_=in_)
             else:
                 nc.scalar.copy(out=out, in_=in_)
 
-        xt = [win.tile([P, 4096], BF16, name="x0", tag="w"), win.tile([P, 4096], BF16, name="x1", tag="w")]
-        w0 = win.tile([P, 4096], BF16, name="w0", tag="w")
+        x_in = [arrive.tile([P, 4096], BF16, name="x%d" % i, tag="in") for i in range(2)]
+        w_in = {0: arrive.tile([P, 4096], BF16, name="w0", tag="in")}
+        w1_rows = W1.rearrange("(g p i e) k -> g e p i k", p=P, i=2, e=2)
+        w2_rows = W2.rearrange("(c p e) k -> c p (e k)", p=P, e=2)
 
         def load_x(rt, lo=0, hi=2048):
-            nc.sync.dma_start(out=xt[rt // 2][:, (rt % 2) * 2048 + lo:(rt % 2) * 2048 + hi], in_=x[rt * P:(rt + 1) * P, lo:hi])
-
-        def load_w0(e):
-            nc.sync.dma_start(out=w0[:].rearrange("p (i k) -> p i k", i=2)[:, :, e * 1024:(e + 1) * 1024], in_=W1.rearrange("(g p i e) k -> g e p i k", p=P, i=2, e=2)[0][0][:, :, e * 1024:(e + 1) * 1024])
+            at = (rt % 2) * 2048
+            nc.sync.dma_start(out=x_in[rt // 2][:, at + lo:at + hi], in_=x[rt * P:(rt + 1) * P, lo:hi])
 
         load_x(0, 0, 1024)
         load_x(0, 1024, 2048)
         ones_b = const.tile([P, 512], BF16, name="ones_b")
         nc.vector.memset(ones_b[:], 1.0)
-        bz = const.tile([P, 512], BF16, name="bz")
-        nc.vector.memset(bz[:], 0.0)
-        nc.sync.dma_start(out=bz[0:4, :], in_=b1.rearrange("(g n) -> g n", n=512))
-        nc.sync.dma_start(out=bz[4:12, 0:256], in_=b2.rearrange("(c n) -> c n", n=256))
+        b_rows = const.tile([P, 512], BF16, name="b_rows")
+        nc.vector.memset(b_rows[:], 0.0)
+        nc.sync.dma_start(out=b_rows[0:4, :], in_=b1.rearrange("(g n) -> g n", n=512))
+        nc.sync.dma_start(out=b_rows[4:12, 0:256], in_=b2.rearrange("(c n) -> c n", n=256))
         load_x(1)
-        load_w0(0)
-        load_w0(1)
+        for half in range(2):
+            cols = slice(half * 1024, (half + 1) * 1024)
+            nc.sync.dma_start(out=w_in[0][:].rearrange("p (i k) -> p i k", i=2)[:, :, cols], in_=w1_rows[0][0][:, :, cols])
         load_x(2)
         load_x(3)
         ident = const.tile([P, P], F32, name="ident")
         make_identity(nc, ident[:])
-        identp = const.tile([P, P], F32, name="identp")
-        nc.gpsimd.tensor_copy(out=identp[:].rearrange("p (u j) -> p u j", u=2), in_=ident[:].rearrange("p (j u) -> p u j", u=2))
+        ident_u = const.tile([P, P], F32, name="ident_u")
+        nc.gpsimd.tensor_copy(out=ident_u[:].rearrange("p (u j) -> p u j", u=2), in_=ident[:].rearrange("p (j u) -> p u j", u=2))
         ones_f = const.tile([P, P], F32, name="ones_f")
         nc.vector.memset(ones_f[:], 1.0)
-        mp = [const.tile([P, 512], F32, name="mp0"), const.tile([P, 256], F32, name="mp1")]
-        nc.vector.memset(mp[0][:], 0.0)
-        nc.gpsimd.memset(mp[1][:], 0.0)
-        tabl = const.tile([P, 1], F32, name="tabl")
-        nc.scalar.activation(out=tabl[:], in_=ones_f[:, 0:1], func=ACT.Relu)
-        warm = psM.tile([P, 512], F32, name="warm", tag="M")
+        vsum1 = const.tile([P, 512], F32, name="vsum1")
+        vsum2 = const.tile([P, 256], F32, name="vsum2")
+        nc.vector.memset(vsum1[:], 0.0)
+        nc.gpsimd.memset(vsum2[:], 0.0)
+        table = const.tile([P, 1], F32, name="table")
+        nc.scalar.activation(out=table[:], in_=ones_f[:, 0:1], func=ACT.Relu)
+        idle = psM.tile([P, 512], F32, name="idle", tag="M")
 
-        def warm_up(n, cols=512):
+        def keep_warm(n):
             for i in range(n):
-                nc.tensor.matmul(out=warm[:, 0:cols], lhsT=ones_b[:, 0:P], rhs=ones_b[:, 0:cols], start=True, stop=True)
+                nc.tensor.matmul(out=idle[:], lhsT=ones_b[:, 0:P], rhs=ones_b[:], start=True, stop=True)
 
-        warm_up(WARM0)
+        keep_warm(4)
 
         gx = const.tile([P, 8192], BF16, name="gx", align_bytes=64)
         xc = const.tile([P, 2048], U32, name="xc", align_bytes=64)
         xsc = const.tile([P, 2048], U8, name="xsc", align_bytes=64)
         hc = const.tile([P, 2048], U32, name="hc", align_bytes=64)
         hsc = const.tile([P, 2048], U8, name="hsc", align_bytes=64)
-        bw = const.tile([P, 16], F32, name="bw")
-        biasf = const.tile([P, 32], F32, name="biasf")
-        sxr = const.tile([P, ROWS], F32, name="sxr")
-        sxp = const.tile([P, 4], F32, name="sxp")
-        sxc = const.tile([P, ROWS], F32, name="sxc")
-        acc = [const.tile([P, ROWS], F32, name="acc0"), const.tile([P, ROWS], F32, name="acc1")]
-        accf = const.tile([P, ROWS], F32, name="accf")
-        shb = const.tile([P, ROWS], F32, name="shb")
-        s1 = const.tile([P, 1], F32, name="s1")
-
-        w1src = W1.rearrange("(g p i e) k -> g e p i k", p=P, i=2, e=2)
-        w2src = W2.rearrange("(c p e) k -> c p (e k)", p=P, e=2)
-        pending = []
-        pw, wt, tb, gw, wc, ws, mb, vt, ob, hcn, gh = {}, {}, {}, {}, {}, {}, {}, {}, {}, {}, {}
+        b_pairs = const.tile([P, 16], F32, name="b_pairs")
+        bias = const.tile([P, 32], F32, name="bias")
+        xsum_cols = const.tile([P, 4], F32, name="xsum_cols")
+        xsum_t = const.tile([P, ROWS], F32, name="xsum_t")
+        xsum = const.tile([P, ROWS], F32, name="xsum")
+        acc = [const.tile([P, ROWS], F32, name="acc%d" % i) for i in range(2)]
+        hsum_p = const.tile([P, ROWS], F32, name="hsum_p")
+        hsum = const.tile([P, ROWS], F32, name="hsum")
+        vsum1_all = const.tile([P, 1], F32, name="vsum1_all")
+        t_bank, gw, wc, wsc, m_bank, v, out_t, hcn, gh, sorted_w, xsum_rep = {}, {}, {}, {}, {}, {}, {}, {}, {}, {}, {}
 
         def load(b):
-            if b <= 15:
-                t = win.tile([P, 4096], BF16, name="w%d" % b, tag="w")
-                if b < 8:
-                    nc.sync.dma_start(out=t[:].rearrange("p (i k) -> p i k", i=2), in_=w1src[b // 2][b % 2])
+            if b < BATCHES:
+                w_in[b] = arrive.tile([P, 4096], BF16, name="w%d" % b, tag="in")
+                if b < FIRST2:
+                    nc.sync.dma_start(out=w_in[b][:].rearrange("p (i k) -> p i k", i=2), in_=w1_rows[b // 2][b % 2])
                 else:
-                    nc.sync.dma_start(out=t[:], in_=w2src[b - 8])
-                wt[b] = t
+                    nc.sync.dma_start(out=w_in[b][:], in_=w2_rows[b - FIRST2])
 
-        def four_transposes(bank, srcs, idn):
+        def four_transposes(name, sources, identity):
+            bank = psT.tile([P, 512], F32, name=name, tag="T")
             for i in range(4):
-                nc.tensor.transpose(out=bank[:, i * P:(i + 1) * P], in_=srcs[i], identity=idn[:])
+                nc.tensor.transpose(out=bank[:, i * P:(i + 1) * P], in_=sources[i], identity=identity[:])
+            return bank
 
-        def pairs(eng, out, in_):
-            copy_on(eng, out.rearrange("p (u n i) -> p u n i", u=2, i=2), in_.rearrange("p (n u i) -> p u n i", u=2, i=2))
+        def sort_pairs(engine, out, in_):
+            copy_on(engine, out.rearrange("p (u n i) -> p u n i", u=2, i=2), in_.rearrange("p (n u i) -> p u n i", u=2, i=2))
 
-        sxrep = {}
-
-        def tx(rt):
-            x32 = xt[rt // 2][:].bitcast(F32)
+        def transpose_x(rt):
+            x32 = x_in[rt // 2][:].bitcast(F32)
             for gp in range(2):
-                bank = psT.tile([P, 512], F32, name="tx%d_%d" % (rt, gp), tag="T")
-                four_transposes(bank, [x32[:, (rt % 2) * 1024 + g * 256 + u:(rt % 2) * 1024 + g * 256 + u + 255:2]
-                                       for g in (2 * gp, 2 * gp + 1) for u in range(2)], ident)
-                tb[("x", rt, gp)] = bank
+                starts = [(rt % 2) * 1024 + g * 256 + u for g in (2 * gp, 2 * gp + 1) for u in range(2)]
+                bank = four_transposes("tx%d_%d" % (rt, gp), [x32[:, at:at + 255:2] for at in starts], ident)
+                t_bank[("x", gp)] = bank
+            for gp in range(2):
+                to = gx[:].bitcast(F32).rearrange("p (g r u) -> p g r u", g=4, u=2)[:, 2 * gp:2 * gp + 2, rt * P:(rt + 1) * P, :]
+                nc.scalar.copy(out=to, in_=t_bank[("x", gp)][:].rearrange("p (g u r) -> p g r u", g=2, u=2))
 
-        def ex(rt, gp, eng):
-            dst = gx[:].bitcast(F32).rearrange("p (g r u) -> p g r u", g=4, u=2)[:, 2 * gp:2 * gp + 2, rt * P:(rt + 1) * P, :]
-            copy_on(eng, dst, tb[("x", rt, gp)][:].rearrange("p (g u r) -> p g r u", g=2, u=2))
-
-        def qx(rt):
-            for g in range(4):
-                lo = g * 512 + rt * P
-                nc.vector.quantize_mx(out=xc[:, lo:lo + P].bitcast(FP8X4), scales=xsc[:, lo:lo + P], in_=gx[:, 4 * lo:4 * (lo + P)])
-
-        def qxh(h):
-            for g in range(4):
-                lo = g * 512 + h * 256
+        def quantise_x(half):
+            for g in range(GROUPS):
+                lo = g * 512 + half * 256
                 nc.vector.quantize_mx(out=xc[:, lo:lo + 256].bitcast(FP8X4), scales=xsc[:, lo:lo + 256], in_=gx[:, 4 * lo:4 * (lo + 256)])
 
-        def sx(rt):
-            if SX[rt] == "P":
-                bank = psT.tile([P, 512], F32, name="sx%d" % rt, tag="T")
-                for g in range(4):
-                    nc.tensor.matmul(out=bank[:], lhsT=ones_b[:, 0:P], rhs=gx[:, g * 2048 + rt * 512:g * 2048 + (rt + 1) * 512],
-                                     start=(g == 0), stop=(g == 3))
-                nc.vector.tensor_reduce(out=sxr[:, rt * P:(rt + 1) * P], in_=bank[:].rearrange("p (r t) -> p r t", t=4),
-                                        axis=AX.X, op=ALU.add)
-            else:
-                junk = stage.tile([P, 2048], BF16, name="jk%d" % rt, tag="pw", bufs=NPW)
-                src = xt[rt // 2][:, (rt % 2) * 2048:(rt % 2) * 2048 + 2048]
-                if SX[rt] == "V":
-                    nc.vector.tensor_scalar(out=junk[:], in0=src, scalar1=1.0, scalar2=0.0, op0=ALU.mult, op1=ALU.add, accum_out=sxp[:, rt:rt + 1])
+        def xsum_rows(rt):
+            unused = stage.tile([P, 2048], BF16, name="unused%d" % rt, tag="sorted", bufs=SORT_BUFS)
+            nc.vector.tensor_scalar(out=unused[:], in0=x_in[rt // 2][:, (rt % 2) * 2048:(rt % 2) * 2048 + 2048], scalar1=1.0, scalar2=0.0,
+                                    op0=ALU.mult, op1=ALU.add, accum_out=xsum_cols[:, rt:rt + 1])
+            xsum_rep[rt] = work.tile([P, P], F32, name="xsum_rep%d" % rt, tag="xsum_rep", bufs=4)
+            nc.gpsimd.tensor_scalar(out=xsum_rep[rt][:], in0=ones_f[:], scalar1=xsum_cols[:, rt:rt + 1], scalar2=C / ROWS,
+                                    op0=ALU.mult, op1=ALU.mult)
+
+        def xsum_matmul(rt):
+            bank = psT.tile([P, 512], F32, name="xs%d" % rt, tag="T")
+            for g in range(GROUPS):
+                at = g * 2048 + rt * 512
+                nc.tensor.matmul(out=bank[:], lhsT=ones_b[:, 0:P], rhs=gx[:, at:at + 512], start=(g == 0), stop=(g == 3))
+            nc.vector.tensor_reduce(out=xsum_t[:, rt * P:(rt + 1) * P], in_=bank[:].rearrange("p (r t) -> p r t", t=4), axis=AX.X, op=ALU.add)
+
+        def spread_xsum():
+            bank = psT.tile([P, 512], F32, name="xsum_bank", tag="T")
+            for rt in range(3):
+                nc.tensor.transpose(out=bank[:, rt * P:(rt + 1) * P], in_=xsum_rep[rt][:], identity=ident[:])
+            for rt in range(3):
+                nc.scalar.copy(out=xsum[:, rt * P:(rt + 1) * P], in_=bank[:, rt * P:(rt + 1) * P])
+            nc.vector.tensor_scalar(out=xsum[:, 3 * P:], in0=xsum_t[:, 3 * P:], scalar1=C / ROWS, scalar2=None, op0=ALU.mult)
+
+        def sort_tile(b):
+            if b not in sorted_w:
+                sorted_w[b] = stage.tile([P, 2048], F32, name="sorted%d" % b, tag="sorted", bufs=SORT_BUFS)
+            return sorted_w[b]
+
+        def sort_on_vector(b, rows=(0, 1)):
+            for e in rows:
+                sort_pairs("V", sort_tile(b)[:, e * 1024:(e + 1) * 1024], w_in[b][:, e * 2048:(e + 1) * 2048].bitcast(F32))
+
+        def sort_quarter_on_scalar(b, n):
+            e, q = n // 2, n % 2
+            copy_on("S", sort_tile(b)[:, e * 1024:(e + 1) * 1024].rearrange("p (u q n i) -> p q u n i", u=2, q=2, i=2)[:, q],
+                    w_in[b][:, n * 1024:(n + 1) * 1024].bitcast(F32).rearrange("p (n u i) -> p u n i", u=2, i=2))
+
+        def transpose_w(b, banks=(0, 1, 2, 3)):
+            w32 = w_in[b][:].bitcast(F32)
+            for n in banks:
+                if b < FIRST2:
+                    starts = [i * 1024 + n * 256 + u for i in range(2) for u in range(2)]
+                    t_bank[(b, n)] = four_transposes("tw%d_%d" % (b, n), [w32[:, at:at + 255:2] for at in starts], ident_u)
                 else:
-                    nc.scalar.activation(out=junk[:], in_=src, func=ACT.Identity, accum_out=sxp[:, rt:rt + 1])
-                sxrep[rt] = work.tile([P, P], F32, name="sxrep%d" % rt, tag="sxrep", bufs=4)
-                nc.gpsimd.tensor_scalar(out=sxrep[rt][:], in0=ones_f[:], scalar1=sxp[:, rt:rt + 1], scalar2=C / ROWS, op0=ALU.mult, op1=ALU.mult)
+                    starts = [n // 2 * 1024 + u * 512 + g * P for g in (n % 2 * 2, n % 2 * 2 + 1) for u in range(2)]
+                    t_bank[(b, n)] = four_transposes("tw%d_%d" % (b, n), [sorted_w[b][:, at:at + P] for at in starts], ident)
 
-        def sx_spread():
-            rts = [rt for rt in range(4) if SX[rt] != "P"]
-            if len(rts) > 0:
-                bank = psT.tile([P, 512], F32, name="sxb", tag="T")
-                for rt in rts:
-                    nc.tensor.transpose(out=bank[:, rt * P:(rt + 1) * P], in_=sxrep[rt][:], identity=ident[:])
-                for rt in rts:
-                    nc.scalar.copy(out=sxc[:, rt * P:(rt + 1) * P], in_=bank[:, rt * P:(rt + 1) * P])
-            for rt in range(4):
-                if SX[rt] == "P":
-                    nc.vector.tensor_scalar(out=sxc[:, rt * P:(rt + 1) * P], in0=sxr[:, rt * P:(rt + 1) * P], scalar1=C / ROWS, scalar2=None, op0=ALU.mult)
-
-        def pw_tile(b):
-            if b not in pw:
-                pw[b] = stage.tile([P, 2048], F32, name="pw%d" % b, tag="pw", bufs=NPW)
-            return pw[b]
-
-        def perm(b):
-            if b >= 8:
-                for e in range(2):
-                    if (b, e) not in QUARTERED:
-                        pairs(PERM.get((b, e), "V"), pw_tile(b)[:, e * 1024:(e + 1) * 1024], wt[b][:, e * 2048:(e + 1) * 2048].bitcast(F32))
-
-        def perm_quarter(b, e, q):
-            copy_on("S", pw_tile(b)[:, e * 1024:(e + 1) * 1024].rearrange("p (u q n i) -> p q u n i", u=2, q=2, i=2)[:, q],
-                    wt[b][:, e * 2048 + q * 1024:e * 2048 + (q + 1) * 1024].bitcast(F32).rearrange("p (n u i) -> p u n i", u=2, i=2))
-
-        def tw(b, which=(0, 1, 2, 3)):
-            w32 = wt[b][:].bitcast(F32)
-
-            def src(g, i, u):
-                if b < 8:
-                    at = i * 1024 + g * 256 + u
-                    return w32[:, at:at + 255:2]
-                at = i * 1024 + u * 512 + g * P
-                return pw[b][:, at:at + P]
-
-            for i in which:
-                bank = psT.tile([P, 512], F32, name="tw%d_%d" % (b, i), tag="T")
-                if b < 8:
-                    four_transposes(bank, [src(i, r, u) for r in range(2) for u in range(2)], identp)
-                else:
-                    e, gp = i // 2, i % 2
-                    four_transposes(bank, [src(g, e, u) for g in (2 * gp, 2 * gp + 1) for u in range(2)], ident)
-                tb[(b, i)] = bank
-
-        def ew(b, i, eng):
-            if i == 0:
+        def gather_w(b, banks=(0, 1, 2, 3)):
+            if b not in gw:
                 gw[b] = stage.tile([P, 4096], BF16, name="gw%d" % b, tag="gw", align_bytes=64)
-            dst = gw[b][:].bitcast(F32)[:, i * 512:(i + 1) * 512]
-            if b < 8:
-                copy_on(eng, dst.rearrange("p (o i u) -> p o i u", i=2, u=2), tb[(b, i)][:].rearrange("p (i u o) -> p o i u", i=2, u=2))
-            else:
-                copy_on(eng, dst.rearrange("p (g o u) -> p g o u", g=2, u=2), tb[(b, i)][:].rearrange("p (g u o) -> p g o u", g=2, u=2))
+            for n in banks:
+                to = gw[b][:].bitcast(F32)[:, n * 512:(n + 1) * 512]
+                if b < FIRST2:
+                    nc.scalar.copy(out=to.rearrange("p (o i u) -> p o i u", i=2, u=2), in_=t_bank[(b, n)][:].rearrange("p (i u o) -> p o i u", i=2, u=2))
+                else:
+                    nc.scalar.copy(out=to.rearrange("p (g o u) -> p g o u", g=2, u=2), in_=t_bank[(b, n)][:].rearrange("p (g u o) -> p g o u", g=2, u=2))
 
-        def qw(b, half=None):
-            if half != 1:
+        def quantise_w(b, lo=0, hi=1024):
+            if b not in wc:
                 wc[b] = stage.tile([P, 1024], U32, name="wc%d" % b, tag="wc", align_bytes=64)
-                ws[b] = stage.tile([P, 1024], U8, name="ws%d" % b, tag="ws", align_bytes=64)
-            if half is None:
-                nc.vector.quantize_mx(out=wc[b][:].bitcast(FP8X4), scales=ws[b][:], in_=gw[b][:])
-            else:
-                lo = half * 512
-                nc.vector.quantize_mx(out=wc[b][:, lo:lo + 512].bitcast(FP8X4), scales=ws[b][:, lo:lo + 512], in_=gw[b][:, 4 * lo:4 * lo + 2048])
+                wsc[b] = stage.tile([P, 1024], U8, name="wsc%d" % b, tag="wsc", align_bytes=64)
+            nc.vector.quantize_mx(out=wc[b][:, lo:hi].bitcast(FP8X4), scales=wsc[b][:, lo:hi], in_=gw[b][:, 4 * lo:4 * hi])
 
-        def mm(b, es=(0, 1), gs=(0, 1, 2, 3)):
-            rc, rs = (xc, xsc) if b < 8 else (hc, hsc)
-            for e in es:
-                if gs[0] == 0:
-                    mb[(b, e)] = psM.tile([P, 512], F32, name="m%d_%d" % (b, e), tag="M")
-                for g in gs:
-                    lo = (g * 2 + e) * P if b < 8 else (e * 4 + g) * P
-                    nc.tensor.matmul_mx(out=mb[(b, e)][:], lhsT=wc[b][:, lo:lo + P].bitcast(FP8X4), lhsT_scale=ws[b][:, lo:lo + P],
-                                        rhs=rc[:, g * 512:(g + 1) * 512].bitcast(FP8X4), rhs_scale=rs[:, g * 512:(g + 1) * 512],
-                                        start=(g == 0), stop=(g == 3))
+        def multiply(b, e, groups=(0, 1, 2, 3), lo=0, hi=ROWS):
+            codes, scales = (xc, xsc) if b < FIRST2 else (hc, hsc)
+            if (b, e) not in m_bank:
+                m_bank[(b, e)] = psM.tile([P, ROWS], F32, name="m%d_%d" % (b, e), tag="M")
+            for g in groups:
+                w_at = (g * 2 + e) * P if b < FIRST2 else (e * 4 + g) * P
+                nc.tensor.matmul_mx(out=m_bank[(b, e)][:, lo:hi], lhsT=wc[b][:, w_at:w_at + P].bitcast(FP8X4), lhsT_scale=wsc[b][:, w_at:w_at + P],
+                                    rhs=codes[:, g * 512 + lo:g * 512 + hi].bitcast(FP8X4), rhs_scale=scales[:, g * 512 + lo:g * 512 + hi],
+                                    start=(g == 0), stop=(g == 3))
 
-        def mm_half(h):
-            for e in range(2):
-                if h == 0:
-                    mb[(0, e)] = psM.tile([P, 512], F32, name="m0_%d" % e, tag="M")
-                for g in range(4):
-                    lo, at = (g * 2 + e) * P, g * 512 + h * 256
-                    nc.tensor.matmul_mx(out=mb[(0, e)][:, h * 256:(h + 1) * 256], lhsT=wc[0][:, lo:lo + P].bitcast(FP8X4),
-                                        lhsT_scale=ws[0][:, lo:lo + P], rhs=xc[:, at:at + 256].bitcast(FP8X4), rhs_scale=xsc[:, at:at + 256],
-                                        start=(g == 0), stop=(g == 3))
+        def row_sum(b, e):
+            if b < FIRST2:
+                at = (2 * e + b % 2) * P + b // 2
+                return vsum1[:, at:at + 1]
+            return vsum2[:, e * P + b - FIRST2:e * P + b - FIRST2 + 1]
 
-        def msum(b, e):
-            col = (2 * e + b % 2) * P + b // 2 if b < 8 else e * P + b - 8
-            return mp[b // 8][:, col:col + 1]
+        def relu(b, e):
+            at = (b // 2 * 2 + e) * 2 + b % 2 if b < FIRST2 else 2 * b + e
+            v[(b, e)] = work.tile([P, ROWS], F32, name="v%d_%d" % (b, e), tag="v", bufs=V_BUFS)
+            nc.scalar.activation(out=v[(b, e)][:], in_=m_bank[(b, e)][:], func=ACT.Relu, bias=bias[:, at:at + 1], scale=1.0,
+                                 accum_out=row_sum(b, e))
 
-        def act(b, e):
-            j = (b // 2 * 2 + e) * 2 + b % 2 if b < 8 else 16 + (b - 8) * 2 + e
-            vt[(b, e)] = work.tile([P, ROWS], F32, name="v%d_%d" % (b, e), tag="v", bufs=NV)
-            nc.scalar.activation(out=vt[(b, e)][:], in_=mb[(b, e)][:], func=ACT.Relu, bias=biasf[:, j:j + 1], scale=1.0,
-                                 accum_out=msum(b, e))
-            if b < 8:
-                pending.append((b, e))
+        tiles1 = [(b, e) for b in range(FIRST2) for e in range(2)]
 
-
-        added = [0]
-
-        def hh(b, e):
-            g, t = b // 2, 2 * e + b % 2
-            if t == 0:
+        def correct_h(b):
+            g = b // 2
+            if b % 2 == 0:
                 hcn[g] = work.tile([P, 2048], BF16, name="hcn%d" % g, tag="hcn")
-            nc.vector.scalar_tensor_tensor(out=hcn[g][:, t * ROWS:(t + 1) * ROWS], in0=sxc[:], scalar=msum(b, e), in1=vt[(b, e)][:],
-                                           op0=ALU.mult, op1=ALU.add)
+            for e in range(2):
+                t = 2 * e + b % 2
+                nc.vector.scalar_tensor_tensor(out=hcn[g][:, t * ROWS:(t + 1) * ROWS], in0=xsum[:], scalar=row_sum(b, e), in1=v[(b, e)][:],
+                                               op0=ALU.mult, op1=ALU.add)
 
-        def adds(n):
-            for i in range(n):
-                a = added[0]
-                if a < 14 and a + 2 < len(pending):
-                    first = vt[pending[a]] if a < 2 else acc[a % 2]
-                    nc.vector.tensor_tensor(out=acc[a % 2][:], in0=first[:], in1=vt[pending[a + 2]][:], op=ALU.add)
-                    added[0] = a + 1
-
-        def rg(g):
+        def gather_h(g):
             gh[g] = work.tile([P, 2048], BF16, name="gh%d" % g, tag="gh", align_bytes=64)
-            nc.vector.tensor_copy(out=gh[g][:].rearrange("p (c i t) -> p c t i", i=4, t=4),
-                                  in_=hcn[g][:].rearrange("p (t c i) -> p c t i", t=4, i=4))
+            nc.vector.tensor_copy(out=gh[g][:].rearrange("p (c i t) -> p c t i", i=4, t=4), in_=hcn[g][:].rearrange("p (t c i) -> p c t i", t=4, i=4))
 
-        def qh(g):
+        def quantise_h(g):
             nc.vector.quantize_mx(out=hc[:, g * 512:(g + 1) * 512].bitcast(FP8X4), scales=hsc[:, g * 512:(g + 1) * 512], in_=gh[g][:])
 
-        def sh_vector():
-            nc.vector.tensor_reduce(out=s1[:], in_=mp[0][:].rearrange("p (t c) -> p t c", t=4)[:, :, 0:4], axis=AX.XY, op=ALU.add)
-            nc.vector.scalar_tensor_tensor(out=accf[:], in0=sxc[:], scalar=s1[:], in1=acc[0][:], op0=ALU.mult, op1=ALU.add)
-            nc.vector.tensor_tensor(out=accf[:], in0=accf[:], in1=acc[1][:], op=ALU.add)
+        def add_v1(n):
+            first = v[tiles1[n]] if n < 2 else acc[n % 2]
+            nc.vector.tensor_tensor(out=acc[n % 2][:], in0=first[:], in1=v[tiles1[n + 2]][:], op=ALU.add)
 
-        def sh_rest():
-            bank = psT.tile([P, 512], F32, name="shb", tag="T")
-            nc.tensor.matmul(out=bank[:], lhsT=ones_f[:], rhs=accf[:], start=True, stop=True)
-            nc.scalar.mul(out=shb[:], in_=bank[:], mul=C / ROWS)
+        def sum_h_tiles():
+            nc.vector.tensor_reduce(out=vsum1_all[:], in_=vsum1[:].rearrange("p (t c) -> p t c", t=4)[:, :, 0:4], axis=AX.XY, op=ALU.add)
+            nc.vector.scalar_tensor_tensor(out=hsum_p[:], in0=xsum[:], scalar=vsum1_all[:], in1=acc[0][:], op0=ALU.mult, op1=ALU.add)
+            nc.vector.tensor_tensor(out=hsum_p[:], in0=hsum_p[:], in1=acc[1][:], op=ALU.add)
 
-        def corr(b, es=(0, 1)):
-            for e in es:
-                nc.vector.scalar_tensor_tensor(out=vt[(b, e)][:], in0=shb[:], scalar=msum(b, e), in1=vt[(b, e)][:], op0=ALU.mult, op1=ALU.add)
+        def spread_hsum():
+            bank = psT.tile([P, ROWS], F32, name="hsum_bank", tag="T")
+            nc.tensor.matmul(out=bank[:], lhsT=ones_f[:], rhs=hsum_p[:], start=True, stop=True)
+            nc.scalar.mul(out=hsum[:], in_=bank[:], mul=C / ROWS)
 
-        def to(b):
-            for k in range(2):
-                tb[("o", b, k)] = psT.tile([P, 512], F32, name="to%d_%d" % (b, k), tag="T")
+        def correct_out(b, e):
+            nc.vector.scalar_tensor_tensor(out=v[(b, e)][:], in0=hsum[:], scalar=row_sum(b, e), in1=v[(b, e)][:], op0=ALU.mult, op1=ALU.add)
+
+        def transpose_out(b):
+            banks = [psT.tile([P, 512], F32, name="to%d_%d" % (b, k), tag="T") for k in range(2)]
             for e in range(2):
-                for rb in range(4):
-                    at = ((rb % 2) * 2 + e) * P
-                    nc.tensor.transpose(out=tb[("o", b, rb // 2)][:, at:at + P], in_=vt[(b, e)][:, rb * P:(rb + 1) * P], identity=ident[:])
+                for rt in range(4):
+                    at = ((rt % 2) * 2 + e) * P
+                    nc.tensor.transpose(out=banks[rt // 2][:, at:at + P], in_=v[(b, e)][:, rt * P:(rt + 1) * P], identity=ident[:])
+            t_bank[("out", b)] = banks
 
-        def eo(b, engines="SS"):
-            c = b - 8
-            ob[b] = work.tile([P, 1024], F32, name="o%d" % b, tag="o", bufs=4)
+        def store(b, engines, halves):
+            lo = (b - FIRST2) * 256
+            rows = out_0.rearrange("(k l r) o -> k r l o", l=2, r=P)
+            out_t[b] = work.tile([P, 1024], F32, name="o%d" % b, tag="o", bufs=OUT_BUFS)
             for k in range(2):
-                copy_on(engines[k], ob[b][:, k * 512:(k + 1) * 512].rearrange("r (l p e) -> r l p e", l=2, e=2),
-                        tb[("o", b, k)][:].rearrange("r (l e p) -> r l p e", l=2, e=2))
-                if b >= 13:
-                    nc.sync.dma_start(out=out_0.rearrange("(k r) o -> r k o", r=P)[:, 2 * k:2 * k + 2, c * 256:(c + 1) * 256],
-                                      in_=ob[b][:, k * 512:(k + 1) * 512].rearrange("r (l o) -> r l o", l=2))
-            if b < 13:
-                nc.sync.dma_start(out=out_0.rearrange("(k r) o -> r k o", r=P)[:, :, c * 256:(c + 1) * 256],
-                                  in_=ob[b][:].rearrange("r (k o) -> r k o", k=4))
+                half = out_t[b][:, k * 512:(k + 1) * 512]
+                copy_on(engines[k], half.rearrange("r (l p e) -> r l p e", l=2, e=2), t_bank[("out", b)][k][:].rearrange("r (l e p) -> r l p e", l=2, e=2))
+                if halves:
+                    nc.sync.dma_start(out=rows[k][:, :, lo:lo + 256], in_=half.rearrange("r (l o) -> r l o", l=2))
+            if not halves:
+                nc.sync.dma_start(out=out_0.rearrange("(k r) o -> r k o", r=P)[:, :, lo:lo + 256], in_=out_t[b][:].rearrange("r (k o) -> r k o", k=4))
 
-        def mout2():
-            bank = psT.tile([P, 512], F32, name="mo2", tag="T")
+        def store_m1():
+            bank = four_transposes("tm1", [vsum1[:, t * P:(t + 1) * P] for t in range(4)], ident)
+            mean = work.tile([P, 512], F32, name="mean1", tag="mean1", bufs=1)
+            to = mean[:].rearrange("c (j u i e) -> c e j u i", u=2, i=2, e=2)
+            sums = bank[:].rearrange("c (u e j i) -> c e j u i", u=2, e=2, i=2)
+            nc.scalar.activation(out=to[:, 0], in_=sums[:, 0], func=ACT.Copy, scale=1.0 / ROWS)
+            nc.vector.tensor_scalar(out=to[:, 1], in0=sums[:, 1], scalar1=1.0 / ROWS, scalar2=None, op0=ALU.mult)
+            nc.sync.dma_start(out=out_1.rearrange("(g n) -> g n", n=512), in_=mean[0:4, :])
+
+        def store_m2():
+            bank = psT.tile([P, 512], F32, name="tm2", tag="T")
             for e in range(2):
-                nc.tensor.transpose(out=bank[:, e * P:(e + 1) * P], in_=mp[1][:, e * P:(e + 1) * P], identity=ident[:])
-            ms2 = work.tile([P, 256], F32, name="ms2", tag="ms2", bufs=1)
-            nc.scalar.activation(out=ms2[:].rearrange("c (p e) -> c p e", e=2), in_=bank[:, 0:256].rearrange("c (e p) -> c p e", e=2),
+                nc.tensor.transpose(out=bank[:, e * P:(e + 1) * P], in_=vsum2[:, e * P:(e + 1) * P], identity=ident[:])
+            mean = work.tile([P, 256], F32, name="mean2", tag="mean2", bufs=1)
+            nc.scalar.activation(out=mean[:].rearrange("c (p e) -> c p e", e=2), in_=bank[:, 0:256].rearrange("c (e p) -> c p e", e=2),
                                  func=ACT.Copy, scale=1.0 / ROWS)
-            nc.sync.dma_start(out=out_2.rearrange("(c n) -> c n", n=256), in_=ms2[0:8, :])
+            nc.sync.dma_start(out=out_2.rearrange("(c n) -> c n", n=256), in_=mean[0:8, :])
 
-        def mout1():
-            bank = psT.tile([P, 512], F32, name="mo", tag="T")
-            for t in range(4):
-                nc.tensor.transpose(out=bank[:, t * P:(t + 1) * P], in_=mp[0][:, t * P:(t + 1) * P], identity=ident[:])
-            ms = work.tile([P, 512], F32, name="ms", tag="ms", bufs=1)
-            for e in range(2):
-                nc.scalar.activation(out=ms[:].rearrange("c (j u i e) -> c e j u i", u=2, i=2, e=2)[:, e],
-                                     in_=bank[:].rearrange("c (u e j i) -> c e j u i", u=2, e=2, i=2)[:, e], func=ACT.Copy, scale=1.0 / ROWS)
-            nc.sync.dma_start(out=out_1.rearrange("(g n) -> g n", n=512), in_=ms[0:4, :])
-
-        wt[0] = w0
-        for b in range(1, NW - 2):
+        for b in range(1, IN_BUFS - 2):
             load(b)
+        b1_sorted = const.tile([P, 256], F32, name="b1_sorted")
+        sort_pairs("V", b1_sorted[:], b_rows[:].bitcast(F32))
+        transpose_x(0)
+        xsum_rows(0)
+        keep_warm(2)
+        bank = psT.tile([P, 512], F32, name="tb", tag="T")
+        for u in range(2):
+            nc.tensor.transpose(out=bank[:, u * P:(u + 1) * P], in_=b1_sorted[:, u * P:(u + 1) * P], identity=ident[:])
+        nc.tensor.transpose(out=bank[:, 2 * P:3 * P], in_=b_rows[:].bitcast(F32)[:, 0:P], identity=ident[:])
+        nc.vector.tensor_copy(out=b_pairs[:, 0:8].rearrange("p (g u) -> p g u", u=2), in_=bank[:, 0:2 * P].rearrange("p (u c) -> p c u", u=2)[:, 0:4, :])
+        nc.vector.tensor_copy(out=b_pairs[:, 8:16], in_=bank[:, 2 * P + 4:2 * P + 12])
+        nc.vector.tensor_copy(out=bias[:], in_=b_pairs[:].bitcast(BF16))
+        transpose_x(1)
+        keep_warm(2)
+        transpose_w(0, (0, 1))
+        gather_w(0, (0, 1))
+        keep_warm(1)
+        quantise_x(0)
+        xsum_rows(1)
+        load(IN_BUFS - 2)
+        transpose_w(0, (2, 3))
+        gather_w(0, (2, 3))
+        keep_warm(1)
+        quantise_w(0, 0, 512)
+        transpose_x(2)
+        keep_warm(1)
+        quantise_w(0, 512, 1024)
+        transpose_x(3)
+        for e in range(2):
+            multiply(0, e, lo=0, hi=256)
+        quantise_x(1)
+        xsum_rows(2)
 
-        def txe(rt, engines):
-            tx(rt)
-            ex(rt, 0, engines[0])
-            ex(rt, 1, engines[1])
-
-        bzp = const.tile([P, 256], F32, name="bzp")
-        pairs("V", bzp[:], bz[:].bitcast(F32))
-        txe(0, HX[0])
-        sx(0)
-        warm_up(WARM1)
-        bank = psT.tile([P, 512], F32, name="tbias", tag="T")
-        for h in range(2):
-            nc.tensor.transpose(out=bank[:, h * P:(h + 1) * P], in_=bzp[:, h * P:(h + 1) * P], identity=ident[:])
-        nc.tensor.transpose(out=bank[:, 2 * P:3 * P], in_=bz[:].bitcast(F32)[:, 0:P], identity=ident[:])
-        nc.vector.tensor_copy(out=bw[:, 0:8].rearrange("p (g h) -> p g h", h=2), in_=bank[:, 0:2 * P].rearrange("p (h c) -> p c h", h=2)[:, 0:4, :])
-        nc.vector.tensor_copy(out=bw[:, 8:16], in_=bank[:, 2 * P + 4:2 * P + 12])
-        nc.vector.tensor_copy(out=biasf[:], in_=bw[:].bitcast(BF16))
-        txe(1, HX[1])
-        warm_up(WA)
-        tw(0, (0, 1))
-        ew(0, 0, HW[0])
-        ew(0, 1, HW[1])
-        warm_up(WB)
-        qxh(0)
-        sx(1)
-        load(NW - 2)
-        tw(0, (2, 3))
-        ew(0, 2, HW[2])
-        ew(0, 3, HW[3])
-        warm_up(WC)
-        qw(0, 0)
-        txe(2, HX[2])
-        warm_up(WD)
-        qw(0, 1)
-        txe(3, HX[3])
-        if SX[3] == "S":
-            sx(3)
-        warm_up(DW)
-        mm_half(0)
-        qxh(1)
-        sx(2)
-
-        done_t, done_q, done_p = 0, 0, 1
-        done_h = 0
-        sh_step = 99
-        corrected = [8]
-        turned = [8]
-        b = 0
-
-        def turn_some():
-            ready = corrected[0]
-            later = []
-            for i in range(TPS):
-                if turned[0] < ready:
-                    to(turned[0])
-                    if b == 15 and i == TPS - 1:
-                        later.append(turned[0])
-                    else:
-                        eo(turned[0])
-                    turned[0] = turned[0] + 1
-            for i in range(TPS):
-                if b >= sh_step + SHL + CL and corrected[0] <= b - 1:
-                    corr(corrected[0])
-                    corrected[0] = corrected[0] + 1
-            if b == 15:
-                corr(15, (0,))
-            for t in later:
-                eo(t, "VV")
-
-        while b <= 15:
+        adds_in_step = {0: 0, 1: 1, 5: 1, 6: 1, 7: 0, 8: 1}
+        added = 0
+        for b in range(BATCHES):
             prev = b - 1
-            ahead = min(15, b + AHEAD[min(b, 19)])
-            t_list = list(range(done_t + 1, ahead + 1))
-            late = t_list[1:] if b == 8 else []
-            if 0 <= prev:
-                act(prev, 1)
-            if not TMID:
-                turn_some()
-            if b == SPREAD:
-                sx_spread()
-            fresh = []
-            for i in range(HHN[b] if b < 9 else 0):
-                n = done_h
-                hh(n // 2, n % 2)
-                done_h = n + 1
-                if n % 4 == 3:
-                    rg(n // 4)
-                    fresh.append(n // 4)
-            if b == 8:
-                qh(3)
-            for t in range(done_q + 1, done_t + 1):
-                qw(t)
-                done_q = t
-            split = SPLIT[b] if 1 <= b <= 15 and b != 8 and len(t_list) == 1 else 0
-            if split:
-                t = t_list[0]
-                tw(t, (0, 1))
-                for i in range(2):
-                    ew(t, i, EWE[t][i])
-            for t in t_list:
-                if t not in late and not split:
-                    tw(t)
-                    if b > 0:
-                        load(t + NW)
-                    done_t = t
-                    for i in range(4):
-                        ew(t, i, EWE[t][i])
-            need_p = min(15, max(ahead, b + 1 + AHEAD[min(b + 1, 19)]))
-            if done_p < need_p:
-                done_p = done_p + 1
-                perm(done_p)
-            if b < 8:
-                for g in fresh:
-                    qh(g)
-            if b == MO:
-                mout1()
+            if b > 0:
+                relu(prev, 1)
+            if b == 1:
+                spread_xsum()
+            if 1 <= b <= FIRST2:
+                correct_h(prev)
+                if prev % 2 == 1:
+                    gather_h(prev // 2)
+            if b == FIRST2:
+                quantise_h(3)
+            if b > FIRST2 and b + 1 < BATCHES:
+                quantise_w(b + 1)
+            ahead = b + 1 if b <= FIRST2 else b + 2
+            if ahead < BATCHES:
+                transpose_w(ahead)
+                if b > 0:
+                    load(ahead + IN_BUFS)
+                gather_w(ahead)
+            if b == FIRST2:
+                for n in (2, 3):
+                    sort_quarter_on_scalar(b + 2, n)
+            sort = b + 2 if b < FIRST2 else b + 3
+            if FIRST2 < sort < BATCHES:
+                sort_on_vector(sort)
+            if 1 < b < FIRST2 and prev % 2 == 1:
+                quantise_h(prev // 2)
             if b == 0:
-                mm_half(1)
-                act(0, 0)
-            elif b == 8:
-                mm(8, (0, 1), (0, 1, 2))
-                for t in late:
-                    tw(t)
-                    load(t + NW)
-                    done_t = t
-                    for i in range(4):
-                        ew(t, i, EWE[t][i])
-                mm(8, (0, 1), (3,))
-                act(8, 0)
-            elif b <= 15:
-                mm(b, (0,))
-                act(b, 0)
-                for qb, qe, qq in SQ.get(b, []):
-                    perm_quarter(qb, qe, qq)
-                if split:
-                    t = t_list[0]
-                    tw(t, (2, 3))
-                    load(t + NW)
-                    done_t = t
-                    for i in range(2, 4):
-                        ew(t, i, EWE[t][i])
-                if TMID:
-                    turn_some()
-                mm(b, (1,))
-            if b == sh_step + SHL:
-                sh_rest()
-            if b + 1 <= 15 and done_q < b + 1:
-                qw(b + 1)
-                done_q = b + 1
+                for e in range(2):
+                    multiply(0, e, lo=256, hi=512)
+                relu(0, 0)
+            elif b == FIRST2:
+                for e in range(2):
+                    multiply(b, e, groups=(0, 1, 2))
+                transpose_w(b + 2)
+                load(b + 2 + IN_BUFS)
+                gather_w(b + 2)
+                for e in range(2):
+                    multiply(b, e, groups=(3,))
+                relu(b, 0)
+            else:
+                multiply(b, 0)
+                relu(b, 0)
+                if 3 <= b < 7:
+                    sort_quarter_on_scalar(FIRST2, b - 3)
+                first = FIRST2 + 2 * (b - CORRECT_FROM)
+                if b > CORRECT_FROM:
+                    for t in (first - 2, first - 1):
+                        transpose_out(t)
+                        if t != LAST - 2:
+                            store(t, "SS", False)
+                if b >= CORRECT_FROM:
+                    for t in (first, first + 1):
+                        for e in range(2):
+                            if (t, e) != (LAST, 1):
+                                correct_out(t, e)
+                if b == LAST:
+                    store(LAST - 2, "VV", True)
+                multiply(b, 1)
+            if b == ADDS_END + 1:
+                spread_hsum()
+            if b <= FIRST2:
+                quantise_w(b + 1)
             if b == 0:
-                if SX[3] != "S":
-                    sx(3)
-                for t in range(NW - 1, done_t + NW + 1):
+                xsum_matmul(3)
+                for t in range(IN_BUFS - 1, IN_BUFS + 2):
                     load(t)
-            while done_p < need_p:
-                done_p = done_p + 1
-                perm(done_p)
-            if sh_step == 99:
-                adds(ADD[b] if b < len(ADD) else 2)
-                if added[0] == 14:
-                    sh_vector()
-                    sh_step = b
-            b = b + 1
+            if b == FIRST2 - 1:
+                sort_on_vector(FIRST2 + 2, (0,))
+            if b <= ADDS_END:
+                for n in range(added, added + adds_in_step.get(b, 2)):
+                    add_v1(n)
+                added = added + adds_in_step.get(b, 2)
+            if b == ADDS_END:
+                sum_h_tiles()
 
-        act(15, 1)
-        last = corrected[0]
-        for t in range(last, 15):
-            corr(t)
-        if ECORR:
-            corr(15, (1,))
-        else:
-            corr(15)
-        for t in range(turned[0], 16):
-            to(t)
-            eo(t, "SV")
-        if MO > 15:
-            mout1()
-        mout2()
+        relu(LAST, 1)
+        correct_out(LAST, 1)
+        for t in (LAST - 1, LAST):
+            transpose_out(t)
+            store(t, "SV", True)
+        store_m2()
+        store_m1()

from contextlib import ExitStack

import concourse.mybir as mybir
from concourse.masks import make_identity

F32 = mybir.dt.float32
BF16 = mybir.dt.bfloat16
U32 = mybir.dt.uint32
U8 = mybir.dt.uint8
FP8X4 = mybir.dt.float8_e4m3fn_x4
ACT = mybir.ActivationFunctionType
ALU = mybir.AluOpType
AX = mybir.AxisListType

P = 128
ROWS = 512
GROUPS = 4
BATCHES = 16
FIRST2 = 8
LAST = BATCHES - 1
C = 0.01 * 0.001 / 1

IN_BUFS = 6
SORT_BUFS = 3
V_BUFS = 16
OUT_BUFS = 4
T_BANKS, M_BANKS = 6, 2

ADDS_END = 10
CORRECT_FROM = 12


def tile_optimalnet_pa_kernel(tc, x, W1, b1, W2, b2, out_0, out_1, out_2):
    nc = tc.nc
    with ExitStack() as ctx:
        const = ctx.enter_context(tc.tile_pool(name="const", bufs=1))
        arrive = ctx.enter_context(tc.tile_pool(name="arrive", bufs=IN_BUFS))
        stage = ctx.enter_context(tc.tile_pool(name="stage", bufs=3))
        work = ctx.enter_context(tc.tile_pool(name="work", bufs=2))
        psT = ctx.enter_context(tc.psum_pool(name="psT", bufs=T_BANKS))
        psM = ctx.enter_context(tc.psum_pool(name="psM", bufs=M_BANKS))
        ctx.enter_context(tc.manual_schedule())

        def copy_on(engine, out, in_):
            if engine == "V":
                nc.vector.tensor_copy(out=out, in_=in_)
            else:
                nc.scalar.copy(out=out, in_=in_)

        x_in = [arrive.tile([P, 4096], BF16, name="x%d" % i, tag="in") for i in range(2)]
        w_in = {0: arrive.tile([P, 4096], BF16, name="w0", tag="in")}
        w1_rows = W1.rearrange("(g p i e) k -> g e p i k", p=P, i=2, e=2)
        w2_rows = W2.rearrange("(c p e) k -> c p (e k)", p=P, e=2)

        def load_x(rt, lo=0, hi=2048):
            at = (rt % 2) * 2048
            nc.sync.dma_start(out=x_in[rt // 2][:, at + lo:at + hi], in_=x[rt * P:(rt + 1) * P, lo:hi])

        load_x(0, 0, 1024)
        load_x(0, 1024, 2048)
        ones_b = const.tile([P, 512], BF16, name="ones_b")
        nc.vector.memset(ones_b[:], 1.0)
        b_rows = const.tile([P, 512], BF16, name="b_rows")
        nc.vector.memset(b_rows[:], 0.0)
        nc.sync.dma_start(out=b_rows[0:4, :], in_=b1.rearrange("(g n) -> g n", n=512))
        nc.sync.dma_start(out=b_rows[4:12, 0:256], in_=b2.rearrange("(c n) -> c n", n=256))
        load_x(1)
        for half in range(2):
            cols = slice(half * 1024, (half + 1) * 1024)
            nc.sync.dma_start(out=w_in[0][:].rearrange("p (i k) -> p i k", i=2)[:, :, cols], in_=w1_rows[0][0][:, :, cols])
        load_x(2)
        load_x(3)
        ident = const.tile([P, P], F32, name="ident")
        make_identity(nc, ident[:])
        ident_u = const.tile([P, P], F32, name="ident_u")
        nc.gpsimd.tensor_copy(out=ident_u[:].rearrange("p (u j) -> p u j", u=2), in_=ident[:].rearrange("p (j u) -> p u j", u=2))
        ones_f = const.tile([P, P], F32, name="ones_f")
        nc.vector.memset(ones_f[:], 1.0)
        vsum1 = const.tile([P, 512], F32, name="vsum1")
        vsum2 = const.tile([P, 256], F32, name="vsum2")
        nc.vector.memset(vsum1[:], 0.0)
        nc.gpsimd.memset(vsum2[:], 0.0)
        table = const.tile([P, 1], F32, name="table")
        nc.scalar.activation(out=table[:], in_=ones_f[:, 0:1], func=ACT.Relu)
        idle = psM.tile([P, 512], F32, name="idle", tag="M")

        def keep_warm(n):
            for i in range(n):
                nc.tensor.matmul(out=idle[:], lhsT=ones_b[:, 0:P], rhs=ones_b[:], start=True, stop=True)

        keep_warm(4)

        gx = const.tile([P, 8192], BF16, name="gx", align_bytes=64)
        xc = const.tile([P, 2048], U32, name="xc", align_bytes=64)
        xsc = const.tile([P, 2048], U8, name="xsc", align_bytes=64)
        hc = const.tile([P, 2048], U32, name="hc", align_bytes=64)
        hsc = const.tile([P, 2048], U8, name="hsc", align_bytes=64)
        b_pairs = const.tile([P, 16], F32, name="b_pairs")
        bias = const.tile([P, 32], F32, name="bias")
        xsum_cols = const.tile([P, 4], F32, name="xsum_cols")
        xsum_t = const.tile([P, ROWS], F32, name="xsum_t")
        xsum = const.tile([P, ROWS], F32, name="xsum")
        acc = [const.tile([P, ROWS], F32, name="acc%d" % i) for i in range(2)]
        hsum_p = const.tile([P, ROWS], F32, name="hsum_p")
        hsum = const.tile([P, ROWS], F32, name="hsum")
        vsum1_all = const.tile([P, 1], F32, name="vsum1_all")
        t_bank, gw, wc, wsc, m_bank, v, out_t, hcn, gh, sorted_w, xsum_rep = {}, {}, {}, {}, {}, {}, {}, {}, {}, {}, {}

        def load(b):
            if b < BATCHES:
                w_in[b] = arrive.tile([P, 4096], BF16, name="w%d" % b, tag="in")
                if b < FIRST2:
                    nc.sync.dma_start(out=w_in[b][:].rearrange("p (i k) -> p i k", i=2), in_=w1_rows[b // 2][b % 2])
                else:
                    nc.sync.dma_start(out=w_in[b][:], in_=w2_rows[b - FIRST2])

        def four_transposes(name, sources, identity):
            bank = psT.tile([P, 512], F32, name=name, tag="T")
            for i in range(4):
                nc.tensor.transpose(out=bank[:, i * P:(i + 1) * P], in_=sources[i], identity=identity[:])
            return bank

        def sort_pairs(engine, out, in_):
            copy_on(engine, out.rearrange("p (u n i) -> p u n i", u=2, i=2), in_.rearrange("p (n u i) -> p u n i", u=2, i=2))

        def transpose_x(rt):
            x32 = x_in[rt // 2][:].bitcast(F32)
            for gp in range(2):
                starts = [(rt % 2) * 1024 + g * 256 + u for g in (2 * gp, 2 * gp + 1) for u in range(2)]
                bank = four_transposes("tx%d_%d" % (rt, gp), [x32[:, at:at + 255:2] for at in starts], ident)
                t_bank[("x", gp)] = bank
            for gp in range(2):
                to = gx[:].bitcast(F32).rearrange("p (g r u) -> p g r u", g=4, u=2)[:, 2 * gp:2 * gp + 2, rt * P:(rt + 1) * P, :]
                nc.scalar.copy(out=to, in_=t_bank[("x", gp)][:].rearrange("p (g u r) -> p g r u", g=2, u=2))

        def quantise_x(half):
            for g in range(GROUPS):
                lo = g * 512 + half * 256
                nc.vector.quantize_mx(out=xc[:, lo:lo + 256].bitcast(FP8X4), scales=xsc[:, lo:lo + 256], in_=gx[:, 4 * lo:4 * (lo + 256)])

        def xsum_rows(rt):
            unused = stage.tile([P, 2048], BF16, name="unused%d" % rt, tag="sorted", bufs=SORT_BUFS)
            nc.vector.tensor_scalar(out=unused[:], in0=x_in[rt // 2][:, (rt % 2) * 2048:(rt % 2) * 2048 + 2048], scalar1=1.0, scalar2=0.0,
                                    op0=ALU.mult, op1=ALU.add, accum_out=xsum_cols[:, rt:rt + 1])
            xsum_rep[rt] = work.tile([P, P], F32, name="xsum_rep%d" % rt, tag="xsum_rep", bufs=4)
            nc.gpsimd.tensor_scalar(out=xsum_rep[rt][:], in0=ones_f[:], scalar1=xsum_cols[:, rt:rt + 1], scalar2=C / ROWS,
                                    op0=ALU.mult, op1=ALU.mult)

        def xsum_matmul(rt):
            bank = psT.tile([P, 512], F32, name="xs%d" % rt, tag="T")
            for g in range(GROUPS):
                at = g * 2048 + rt * 512
                nc.tensor.matmul(out=bank[:], lhsT=ones_b[:, 0:P], rhs=gx[:, at:at + 512], start=(g == 0), stop=(g == 3))
            nc.vector.tensor_reduce(out=xsum_t[:, rt * P:(rt + 1) * P], in_=bank[:].rearrange("p (r t) -> p r t", t=4), axis=AX.X, op=ALU.add)

        def spread_xsum():
            bank = psT.tile([P, 512], F32, name="xsum_bank", tag="T")
            for rt in range(3):
                nc.tensor.transpose(out=bank[:, rt * P:(rt + 1) * P], in_=xsum_rep[rt][:], identity=ident[:])
            for rt in range(3):
                nc.scalar.copy(out=xsum[:, rt * P:(rt + 1) * P], in_=bank[:, rt * P:(rt + 1) * P])
            nc.vector.tensor_scalar(out=xsum[:, 3 * P:], in0=xsum_t[:, 3 * P:], scalar1=C / ROWS, scalar2=None, op0=ALU.mult)

        def sort_tile(b):
            if b not in sorted_w:
                sorted_w[b] = stage.tile([P, 2048], F32, name="sorted%d" % b, tag="sorted", bufs=SORT_BUFS)
            return sorted_w[b]

        def sort_on_vector(b, rows=(0, 1)):
            for e in rows:
                sort_pairs("V", sort_tile(b)[:, e * 1024:(e + 1) * 1024], w_in[b][:, e * 2048:(e + 1) * 2048].bitcast(F32))

        def sort_quarter_on_scalar(b, n):
            e, q = n // 2, n % 2
            copy_on("S", sort_tile(b)[:, e * 1024:(e + 1) * 1024].rearrange("p (u q n i) -> p q u n i", u=2, q=2, i=2)[:, q],
                    w_in[b][:, n * 1024:(n + 1) * 1024].bitcast(F32).rearrange("p (n u i) -> p u n i", u=2, i=2))

        def transpose_w(b, banks=(0, 1, 2, 3)):
            w32 = w_in[b][:].bitcast(F32)
            for n in banks:
                if b < FIRST2:
                    starts = [i * 1024 + n * 256 + u for i in range(2) for u in range(2)]
                    t_bank[(b, n)] = four_transposes("tw%d_%d" % (b, n), [w32[:, at:at + 255:2] for at in starts], ident_u)
                else:
                    starts = [n // 2 * 1024 + u * 512 + g * P for g in (n % 2 * 2, n % 2 * 2 + 1) for u in range(2)]
                    t_bank[(b, n)] = four_transposes("tw%d_%d" % (b, n), [sorted_w[b][:, at:at + P] for at in starts], ident)

        def gather_w(b, banks=(0, 1, 2, 3)):
            if b not in gw:
                gw[b] = stage.tile([P, 4096], BF16, name="gw%d" % b, tag="gw", align_bytes=64)
            for n in banks:
                to = gw[b][:].bitcast(F32)[:, n * 512:(n + 1) * 512]
                if b < FIRST2:
                    nc.scalar.copy(out=to.rearrange("p (o i u) -> p o i u", i=2, u=2), in_=t_bank[(b, n)][:].rearrange("p (i u o) -> p o i u", i=2, u=2))
                else:
                    nc.scalar.copy(out=to.rearrange("p (g o u) -> p g o u", g=2, u=2), in_=t_bank[(b, n)][:].rearrange("p (g u o) -> p g o u", g=2, u=2))

        def quantise_w(b, lo=0, hi=1024):
            if b not in wc:
                wc[b] = stage.tile([P, 1024], U32, name="wc%d" % b, tag="wc", align_bytes=64)
                wsc[b] = stage.tile([P, 1024], U8, name="wsc%d" % b, tag="wsc", align_bytes=64)
            nc.vector.quantize_mx(out=wc[b][:, lo:hi].bitcast(FP8X4), scales=wsc[b][:, lo:hi], in_=gw[b][:, 4 * lo:4 * hi])

        def multiply(b, e, groups=(0, 1, 2, 3), lo=0, hi=ROWS):
            codes, scales = (xc, xsc) if b < FIRST2 else (hc, hsc)
            if (b, e) not in m_bank:
                m_bank[(b, e)] = psM.tile([P, ROWS], F32, name="m%d_%d" % (b, e), tag="M")
            for g in groups:
                w_at = (g * 2 + e) * P if b < FIRST2 else (e * 4 + g) * P
                nc.tensor.matmul_mx(out=m_bank[(b, e)][:, lo:hi], lhsT=wc[b][:, w_at:w_at + P].bitcast(FP8X4), lhsT_scale=wsc[b][:, w_at:w_at + P],
                                    rhs=codes[:, g * 512 + lo:g * 512 + hi].bitcast(FP8X4), rhs_scale=scales[:, g * 512 + lo:g * 512 + hi],
                                    start=(g == 0), stop=(g == 3))

        def row_sum(b, e):
            if b < FIRST2:
                at = (2 * e + b % 2) * P + b // 2
                return vsum1[:, at:at + 1]
            return vsum2[:, e * P + b - FIRST2:e * P + b - FIRST2 + 1]

        def relu(b, e):
            at = (b // 2 * 2 + e) * 2 + b % 2 if b < FIRST2 else 2 * b + e
            v[(b, e)] = work.tile([P, ROWS], F32, name="v%d_%d" % (b, e), tag="v", bufs=V_BUFS)
            nc.scalar.activation(out=v[(b, e)][:], in_=m_bank[(b, e)][:], func=ACT.Relu, bias=bias[:, at:at + 1], scale=1.0,
                                 accum_out=row_sum(b, e))

        tiles1 = [(b, e) for b in range(FIRST2) for e in range(2)]

        def correct_h(b):
            g = b // 2
            if b % 2 == 0:
                hcn[g] = work.tile([P, 2048], BF16, name="hcn%d" % g, tag="hcn")
            for e in range(2):
                t = 2 * e + b % 2
                nc.vector.scalar_tensor_tensor(out=hcn[g][:, t * ROWS:(t + 1) * ROWS], in0=xsum[:], scalar=row_sum(b, e), in1=v[(b, e)][:],
                                               op0=ALU.mult, op1=ALU.add)

        def gather_h(g):
            gh[g] = work.tile([P, 2048], BF16, name="gh%d" % g, tag="gh", align_bytes=64)
            nc.vector.tensor_copy(out=gh[g][:].rearrange("p (c i t) -> p c t i", i=4, t=4), in_=hcn[g][:].rearrange("p (t c i) -> p c t i", t=4, i=4))

        def quantise_h(g):
            nc.vector.quantize_mx(out=hc[:, g * 512:(g + 1) * 512].bitcast(FP8X4), scales=hsc[:, g * 512:(g + 1) * 512], in_=gh[g][:])

        def add_v1(n):
            first = v[tiles1[n]] if n < 2 else acc[n % 2]
            nc.vector.tensor_tensor(out=acc[n % 2][:], in0=first[:], in1=v[tiles1[n + 2]][:], op=ALU.add)

        def sum_h_tiles():
            nc.vector.tensor_reduce(out=vsum1_all[:], in_=vsum1[:].rearrange("p (t c) -> p t c", t=4)[:, :, 0:4], axis=AX.XY, op=ALU.add)
            nc.vector.scalar_tensor_tensor(out=hsum_p[:], in0=xsum[:], scalar=vsum1_all[:], in1=acc[0][:], op0=ALU.mult, op1=ALU.add)
            nc.vector.tensor_tensor(out=hsum_p[:], in0=hsum_p[:], in1=acc[1][:], op=ALU.add)

        def spread_hsum():
            bank = psT.tile([P, ROWS], F32, name="hsum_bank", tag="T")
            nc.tensor.matmul(out=bank[:], lhsT=ones_f[:], rhs=hsum_p[:], start=True, stop=True)
            nc.scalar.mul(out=hsum[:], in_=bank[:], mul=C / ROWS)

        def correct_out(b, e):
            nc.vector.scalar_tensor_tensor(out=v[(b, e)][:], in0=hsum[:], scalar=row_sum(b, e), in1=v[(b, e)][:], op0=ALU.mult, op1=ALU.add)

        def transpose_out(b):
            banks = [psT.tile([P, 512], F32, name="to%d_%d" % (b, k), tag="T") for k in range(2)]
            for e in range(2):
                for rt in range(4):
                    at = ((rt % 2) * 2 + e) * P
                    nc.tensor.transpose(out=banks[rt // 2][:, at:at + P], in_=v[(b, e)][:, rt * P:(rt + 1) * P], identity=ident[:])
            t_bank[("out", b)] = banks

        def store(b, engines, halves):
            lo = (b - FIRST2) * 256
            rows = out_0.rearrange("(k l r) o -> k r l o", l=2, r=P)
            out_t[b] = work.tile([P, 1024], F32, name="o%d" % b, tag="o", bufs=OUT_BUFS)
            for k in range(2):
                half = out_t[b][:, k * 512:(k + 1) * 512]
                copy_on(engines[k], half.rearrange("r (l p e) -> r l p e", l=2, e=2), t_bank[("out", b)][k][:].rearrange("r (l e p) -> r l p e", l=2, e=2))
                if halves:
                    nc.sync.dma_start(out=rows[k][:, :, lo:lo + 256], in_=half.rearrange("r (l o) -> r l o", l=2))
            if not halves:
                nc.sync.dma_start(out=out_0.rearrange("(k r) o -> r k o", r=P)[:, :, lo:lo + 256], in_=out_t[b][:].rearrange("r (k o) -> r k o", k=4))

        def store_m1():
            bank = four_transposes("tm1", [vsum1[:, t * P:(t + 1) * P] for t in range(4)], ident)
            mean = work.tile([P, 512], F32, name="mean1", tag="mean1", bufs=1)
            to = mean[:].rearrange("c (j u i e) -> c e j u i", u=2, i=2, e=2)
            sums = bank[:].rearrange("c (u e j i) -> c e j u i", u=2, e=2, i=2)
            nc.scalar.activation(out=to[:, 0], in_=sums[:, 0], func=ACT.Copy, scale=1.0 / ROWS)
            nc.vector.tensor_scalar(out=to[:, 1], in0=sums[:, 1], scalar1=1.0 / ROWS, scalar2=None, op0=ALU.mult)
            nc.sync.dma_start(out=out_1.rearrange("(g n) -> g n", n=512), in_=mean[0:4, :])

        def store_m2():
            bank = psT.tile([P, 512], F32, name="tm2", tag="T")
            for e in range(2):
                nc.tensor.transpose(out=bank[:, e * P:(e + 1) * P], in_=vsum2[:, e * P:(e + 1) * P], identity=ident[:])
            mean = work.tile([P, 256], F32, name="mean2", tag="mean2", bufs=1)
            nc.scalar.activation(out=mean[:].rearrange("c (p e) -> c p e", e=2), in_=bank[:, 0:256].rearrange("c (e p) -> c p e", e=2),
                                 func=ACT.Copy, scale=1.0 / ROWS)
            nc.sync.dma_start(out=out_2.rearrange("(c n) -> c n", n=256), in_=mean[0:8, :])

        for b in range(1, IN_BUFS - 2):
            load(b)
        b1_sorted = const.tile([P, 256], F32, name="b1_sorted")
        sort_pairs("V", b1_sorted[:], b_rows[:].bitcast(F32))
        transpose_x(0)
        xsum_rows(0)
        keep_warm(2)
        bank = psT.tile([P, 512], F32, name="tb", tag="T")
        for u in range(2):
            nc.tensor.transpose(out=bank[:, u * P:(u + 1) * P], in_=b1_sorted[:, u * P:(u + 1) * P], identity=ident[:])
        nc.tensor.transpose(out=bank[:, 2 * P:3 * P], in_=b_rows[:].bitcast(F32)[:, 0:P], identity=ident[:])
        nc.vector.tensor_copy(out=b_pairs[:, 0:8].rearrange("p (g u) -> p g u", u=2), in_=bank[:, 0:2 * P].rearrange("p (u c) -> p c u", u=2)[:, 0:4, :])
        nc.vector.tensor_copy(out=b_pairs[:, 8:16], in_=bank[:, 2 * P + 4:2 * P + 12])
        nc.vector.tensor_copy(out=bias[:], in_=b_pairs[:].bitcast(BF16))
        transpose_x(1)
        keep_warm(2)
        transpose_w(0, (0, 1))
        gather_w(0, (0, 1))
        keep_warm(1)
        quantise_x(0)
        xsum_rows(1)
        load(IN_BUFS - 2)
        transpose_w(0, (2, 3))
        gather_w(0, (2, 3))
        keep_warm(1)
        quantise_w(0, 0, 512)
        transpose_x(2)
        keep_warm(1)
        quantise_w(0, 512, 1024)
        transpose_x(3)
        for e in range(2):
            multiply(0, e, lo=0, hi=256)
        quantise_x(1)
        xsum_rows(2)

        adds_in_step = {0: 0, 1: 1, 5: 1, 6: 1, 7: 0, 8: 1}
        added = 0
        for b in range(BATCHES):
            prev = b - 1
            if b > 0:
                relu(prev, 1)
            if b == 1:
                spread_xsum()
            if 1 <= b <= FIRST2:
                correct_h(prev)
                if prev % 2 == 1:
                    gather_h(prev // 2)
            if b == FIRST2:
                quantise_h(3)
            if b > FIRST2 and b + 1 < BATCHES:
                quantise_w(b + 1)
            ahead = b + 1 if b <= FIRST2 else b + 2
            if ahead < BATCHES:
                transpose_w(ahead)
                if b > 0:
                    load(ahead + IN_BUFS)
                gather_w(ahead)
            if b == FIRST2:
                for n in (2, 3):
                    sort_quarter_on_scalar(b + 2, n)
            sort = b + 2 if b < FIRST2 else b + 3
            if FIRST2 < sort < BATCHES:
                sort_on_vector(sort)
            if 1 < b < FIRST2 and prev % 2 == 1:
                quantise_h(prev // 2)
            if b == 0:
                for e in range(2):
                    multiply(0, e, lo=256, hi=512)
                relu(0, 0)
            elif b == FIRST2:
                for e in range(2):
                    multiply(b, e, groups=(0, 1, 2))
                transpose_w(b + 2)
                load(b + 2 + IN_BUFS)
                gather_w(b + 2)
                for e in range(2):
                    multiply(b, e, groups=(3,))
                relu(b, 0)
            else:
                multiply(b, 0)
                relu(b, 0)
                if 3 <= b < 7:
                    sort_quarter_on_scalar(FIRST2, b - 3)
                first = FIRST2 + 2 * (b - CORRECT_FROM)
                if b > CORRECT_FROM:
                    for t in (first - 2, first - 1):
                        transpose_out(t)
                        if t != LAST - 2:
                            store(t, "SS", False)
                if b >= CORRECT_FROM:
                    for t in (first, first + 1):
                        for e in range(2):
                            if (t, e) != (LAST, 1):
                                correct_out(t, e)
                if b == LAST:
                    store(LAST - 2, "VV", True)
                multiply(b, 1)
            if b == ADDS_END + 1:
                spread_hsum()
            if b <= FIRST2:
                quantise_w(b + 1)
            if b == 0:
                xsum_matmul(3)
                for t in range(IN_BUFS - 1, IN_BUFS + 2):
                    load(t)
            if b == FIRST2 - 1:
                sort_on_vector(FIRST2 + 2, (0,))
            if b <= ADDS_END:
                for n in range(added, added + adds_in_step.get(b, 2)):
                    add_v1(n)
                added = added + adds_in_step.get(b, 2)
            if b == ADDS_END:
                sum_h_tiles()

        relu(LAST, 1)
        correct_out(LAST, 1)
        for t in (LAST - 1, LAST):
            transpose_out(t)
            store(t, "SV", True)
        store_m2()
        store_m1()
